import numpy as np
import ml_dtypes


def mxq(x, axis, fmt="e4m3"):
    dtype, down = {"e4m3": (ml_dtypes.float8_e4m3fn, 7), "e5m2": (ml_dtypes.float8_e5m2, 14)}[fmt]
    v = np.moveaxis(np.asarray(x, np.float32).astype(ml_dtypes.bfloat16).astype(np.float64), axis, -1)
    blocks = v.reshape(v.shape[:-1] + (-1, 32))
    amax = np.abs(blocks).max(-1, keepdims=True)
    byte = np.maximum(np.where(amax > 0, np.frexp(amax)[1] - 1 + 127, 0) - down, 1)
    scale = np.exp2(byte - 127.0)
    codes = (blocks / scale).astype(np.float32).astype(dtype).astype(np.float64)
    return np.moveaxis((codes * scale).reshape(v.shape), -1, axis)


BF16 = ml_dtypes.bfloat16


def bf(x):
    return np.asarray(x, np.float32).astype(BF16)


def f64(x):
    return np.asarray(x).astype(np.float64)


B, C, HI, WI, H_BINS = 16, 3, 224, 224, 64
EPS = 1e-6
SIGMA = 0.02


def setup_inputs():
    return {"x": bf(np.random.uniform(-0.25, 1.25, (B, C, HI, WI)))}


def reference(x):
    x = np.clip(f64(x), 0.0, 1.0)
    I = x[:, :C].reshape(B, C, -1).transpose(0, 2, 1)
    s = np.sum(I, axis=-1) + EPS
    Ir = I[:, :, 0] / s
    Ig = I[:, :, 1] / s
    bins = np.linspace(0.0, 1.0, H_BINS)
    kr = 1.0 / (1.0 + ((Ir[:, :, None] - bins) / SIGMA) ** 2)
    kg = 1.0 / (1.0 + ((Ig[:, :, None] - bins) / SIGMA) ** 2)
    krq = mxq(kr, 1, "e4m3")
    kgq = mxq(kg, 1, "e4m3")
    hists = (krq.transpose(0, 2, 1) @ kgq)[:, None, :, :]
    norm = np.sum(hists, axis=(1, 2, 3), keepdims=True) + EPS
    return hists / norm

@@ -1,0 +1,179 @@
+from contextlib import ExitStack
+
+import concourse.mybir as mybir
+
+F32 = mybir.dt.float32
+BF16 = mybir.dt.bfloat16
+I32 = mybir.dt.int32
+U32 = mybir.dt.uint32
+U8 = mybir.dt.uint8
+FP8X4 = mybir.dt.float8_e4m3fn_x4
+ALU = mybir.AluOpType
+ACTF = mybir.ActivationFunctionType
+AX = mybir.AxisListType
+
+P = 128
+IMAGES = 16
+PIXELS = 224 * 224
+BINS = 64
+EPS = 1e-6
+SIGMA = 0.02
+SLOTS = PIXELS // P
+PASSES = SLOTS // 4
+GP = 8
+GROUPS = IMAGES * PASSES // GP
+BLKS = 2 * GP
+GCOLS = BLKS * BINS
+S2 = (63.0 * SIGMA) ** 2
+NV = 5
+
+FLOPS = 2 * IMAGES * PIXELS * BINS * BINS
+
+
+def tile_rgchromahistblock_kernel(tc, x, out):
+    nc = tc.nc
+    xv = x.rearrange("b c h w -> b c (h w)").rearrange("b c (p t) -> p b c t", p=P)
+    outv = out.rearrange("b o i j -> i (b o) j")
+    with ExitStack() as ctx:
+        const = ctx.enter_context(tc.tile_pool(name="const", bufs=1))
+        xin = ctx.enter_context(tc.tile_pool(name="xin", bufs=3))
+        prep = ctx.enter_context(tc.tile_pool(name="prep", bufs=2))
+        napool = ctx.enter_context(tc.tile_pool(name="napool", bufs=3))
+        wpool = ctx.enter_context(tc.tile_pool(name="wpool", bufs=3))
+        upool = ctx.enter_context(tc.tile_pool(name="upool", bufs=2))
+        qpool = ctx.enter_context(tc.tile_pool(name="qpool", bufs=3))
+        kpool = ctx.enter_context(tc.tile_pool(name="kpool", bufs=3))
+        cpool = ctx.enter_context(tc.tile_pool(name="cpool", bufs=2))
+        small = ctx.enter_context(tc.tile_pool(name="small", bufs=2))
+        accp = ctx.enter_context(tc.psum_pool(name="accp", bufs=1))
+        totp = ctx.enter_context(tc.psum_pool(name="totp", bufs=2))
+        ctx.enter_context(tc.manual_schedule())
+
+        ji = const.tile([P, BINS], I32)
+        nc.gpsimd.iota(out=ji[:], pattern=[[1, BINS]], base=0, channel_multiplier=0)
+        jf = const.tile([P, BINS], F32)
+        nc.vector.tensor_copy(out=jf[:], in_=ji[:])
+        one = const.tile([P, 1], F32)
+        nc.vector.memset(one[:], 1.0)
+        sel = const.tile([P, P], F32)
+        nc.vector.memset(sel[0:64, :], 1.0)
+        nc.vector.memset(sel[64:128, :], 0.0)
+        acc = [accp.tile([P, 512], F32, name="acc%d" % i) for i in range(4)]
+
+        xt = {}
+        na = {}
+        wt = {}
+        qt = {}
+        kt = {}
+
+        def load(b):
+            xb = xin.tile([P, 3, SLOTS], BF16)
+            nc.sync.dma_start(out=xb[:], in_=xv[:, b])
+            xt[b] = xb
+
+        def prepare(b):
+            cl = prep.tile([P, 3, SLOTS], BF16)
+            nc.vector.tensor_scalar(out=cl[:], in0=xt[b][:], scalar1=0.0, scalar2=1.0, op0=ALU.max, op1=ALU.min)
+            s1 = prep.tile([P, SLOTS], F32)
+            nc.vector.scalar_tensor_tensor(out=s1[:], in0=cl[:, 0, :], scalar=EPS, in1=cl[:, 1, :], op0=ALU.add, op1=ALU.add)
+            s2 = prep.tile([P, SLOTS], F32)
+            nc.vector.tensor_tensor(out=s2[:], in0=s1[:], in1=cl[:, 2, :], op=ALU.add)
+            rs = prep.tile([P, SLOTS], F32)
+            nc.vector.reciprocal(out=rs[:], in_=s2[:])
+            nab = napool.tile([P, 2, SLOTS], F32)
+            nc.vector.scalar_tensor_tensor(
+                out=nab[:], in0=cl[:, 0:2, :], scalar=-63.0,
+                in1=rs[:].unsqueeze(1).to_broadcast([P, 2, SLOTS]), op0=ALU.mult, op1=ALU.mult)
+            na[b] = nab
+
+        def shift(g, blk, j):
+            c, ch = divmod(blk, 2)
+            b, t = divmod(4 * (GP * g + c) + j, SLOTS)
+            return na[b][:, ch, t:t + 1]
+
+        def stage_a(g):
+            w = wpool.tile([P, 4, GCOLS], F32)
+            wt[g] = w
+            na_blks = BLKS - NV
+            for blk in range(na_blks):
+                for j in range(4):
+                    nc.scalar.activation(out=w[:, j, blk * BINS:(blk + 1) * BINS], in_=jf[:], func=ACTF.Square,
+                                         bias=shift(g, blk, j), scale=1.0)
+            u = upool.tile([P, 4, NV * BINS], F32)
+            for k in range(NV):
+                for j in range(4):
+                    nc.vector.tensor_scalar(out=u[:, j, k * BINS:(k + 1) * BINS], in0=jf[:],
+                                            scalar1=shift(g, na_blks + k, j), scalar2=None, op0=ALU.add)
+            nc.vector.tensor_tensor(out=w[:, :, na_blks * BINS:], in0=u[:], in1=u[:], op=ALU.mult)
+
+        def stage_b(g):
+            q = qpool.tile([P, 4 * GCOLS], F32)
+            qt[g] = q
+            wv = wt[g][:].rearrange("p j n -> p n j")
+            nc.vector.scalar_tensor_tensor(out=q[:].rearrange("p (n j) -> p n j", j=4), in0=wv, scalar=2.0 * S2,
+                                           in1=wv, op0=ALU.add, op1=ALU.mult)
+
+        def stage_c(g):
+            k = kpool.tile([P, 4 * GCOLS], BF16, align_bytes=64)
+            kt[g] = k
+            nc.scalar.activation(out=k[:], in_=qt[g][:], func=ACTF.Abs_reciprocal_sqrt, bias=one[:],
+                                 scale=1.0 / (S2 * S2))
+
+        def finish(kb):
+            hist = acc[kb][:].rearrange("p (i c) -> p i c", c=P)[:, :, BINS:P]
+            rsum = small.tile([P, 4], F32)
+            nc.vector.tensor_reduce(out=rsum[:], in_=hist, axis=AX.X, op=ALU.add)
+            tot = totp.tile([P, 4], F32)
+            nc.tensor.matmul(out=tot[:], lhsT=sel[:], rhs=rsum[:], start=True, stop=True)
+            te = small.tile([P, 4], F32)
+            nc.vector.tensor_scalar(out=te[:], in0=tot[:], scalar1=EPS, scalar2=None, op0=ALU.add)
+            rt = small.tile([P, 4], F32)
+            nc.vector.reciprocal(out=rt[:], in_=te[:])
+            o = small.tile([BINS, 4, BINS], F32)
+            nc.vector.tensor_tensor(out=o[:], in0=hist[0:BINS], in1=rt[0:BINS, :].unsqueeze(2).to_broadcast([BINS, 4, BINS]),
+                                    op=ALU.mult)
+            nc.sync.dma_start(out=outv[:, 4 * kb:4 * kb + 4, :], in_=o[:])
+
+        def stage_q(g):
+            codes = cpool.tile([P, GCOLS], U32, align_bytes=64)
+            scales = cpool.tile([P, GCOLS], U8, align_bytes=64)
+            nc.vector.quantize_mx(out=codes[:].bitcast(FP8X4), scales=scales[:], in_=kt[g][:])
+            done = []
+            for c in range(GP):
+                b, cc = divmod(GP * g + c, PASSES)
+                cols = slice(c * P, (c + 1) * P)
+                nc.tensor.matmul_mx(
+                    out=acc[b // 4][:, (b % 4) * P:(b % 4 + 1) * P],
+                    lhsT=codes[:, cols].bitcast(FP8X4), lhsT_scale=scales[:, cols],
+                    rhs=codes[:, cols].bitcast(FP8X4), rhs_scale=scales[:, cols],
+                    start=(cc == 0), stop=(cc == PASSES - 1))
+                if cc == PASSES - 1 and b % 4 == 3:
+                    done.append(b // 4)
+            return done
+
+        first_group = [(b * SLOTS) // (4 * GP) for b in range(IMAGES)]
+        load(0)
+        load(1)
+        load(2)
+        prepare(0)
+        prepared = 1
+        pending = []
+        for n in range(-1, GROUPS + 2):
+            while prepared < IMAGES and first_group[prepared] <= n + 4:
+                if prepared + 2 < IMAGES:
+                    load(prepared + 2)
+                prepare(prepared)
+                prepared += 1
+            if n + 1 < GROUPS:
+                stage_a(n + 1)
+            if 0 <= n < GROUPS:
+                stage_b(n)
+            if 0 <= n - 1 < GROUPS:
+                stage_c(n - 1)
+            for kb in pending:
+                finish(kb)
+            pending = []
+            if 0 <= n - 2:
+                pending = stage_q(n - 2)
+        for kb in pending:
+            finish(kb)

@@ -20,12 +20,15 @@ EPS = 1e-6
 SIGMA = 0.02
 SLOTS = PIXELS // P
 PASSES = SLOTS // 4
-GP = 8
-GROUPS = IMAGES * PASSES // GP
+GP = 14
+GPI = PASSES // GP
+GROUPS = IMAGES * GPI
+GS = 4 * GP
 BLKS = 2 * GP
 GCOLS = BLKS * BINS
 S2 = (63.0 * SIGMA) ** 2
-NV = 5
+WA = 44
+QW = (1024, 512, 256)
 
 FLOPS = 2 * IMAGES * PIXELS * BINS * BINS
 
@@ -38,10 +41,8 @@ def tile_rgchromahistblock_kernel(tc, x, out):
         const = ctx.enter_context(tc.tile_pool(name="const", bufs=1))
         xin = ctx.enter_context(tc.tile_pool(name="xin", bufs=3))
         prep = ctx.enter_context(tc.tile_pool(name="prep", bufs=2))
-        napool = ctx.enter_context(tc.tile_pool(name="napool", bufs=3))
+        napool = ctx.enter_context(tc.tile_pool(name="napool", bufs=6))
         wpool = ctx.enter_context(tc.tile_pool(name="wpool", bufs=3))
-        upool = ctx.enter_context(tc.tile_pool(name="upool", bufs=2))
-        qpool = ctx.enter_context(tc.tile_pool(name="qpool", bufs=3))
         kpool = ctx.enter_context(tc.tile_pool(name="kpool", bufs=3))
         cpool = ctx.enter_context(tc.tile_pool(name="cpool", bufs=2))
         small = ctx.enter_context(tc.tile_pool(name="small", bufs=2))
@@ -51,8 +52,8 @@ def tile_rgchromahistblock_kernel(tc, x, out):
 
         ji = const.tile([P, BINS], I32)
         nc.gpsimd.iota(out=ji[:], pattern=[[1, BINS]], base=0, channel_multiplier=0)
-        jf = const.tile([P, BINS], F32)
-        nc.vector.tensor_copy(out=jf[:], in_=ji[:])
+        negj = const.tile([P, BINS], F32)
+        nc.vector.tensor_scalar(out=negj[:], in0=ji[:], scalar1=-1.0, scalar2=None, op0=ALU.mult)
         one = const.tile([P, 1], F32)
         nc.vector.memset(one[:], 1.0)
         sel = const.tile([P, P], F32)
@@ -63,7 +64,6 @@ def tile_rgchromahistblock_kernel(tc, x, out):
         xt = {}
         na = {}
         wt = {}
-        qt = {}
         kt = {}
 
         def load(b):
@@ -71,53 +71,58 @@ def tile_rgchromahistblock_kernel(tc, x, out):
             nc.sync.dma_start(out=xb[:], in_=xv[:, b])
             xt[b] = xb
 
-        def prepare(b):
-            cl = prep.tile([P, 3, SLOTS], BF16)
-            nc.vector.tensor_scalar(out=cl[:], in0=xt[b][:], scalar1=0.0, scalar2=1.0, op0=ALU.max, op1=ALU.min)
-            s1 = prep.tile([P, SLOTS], F32)
-            nc.vector.scalar_tensor_tensor(out=s1[:], in0=cl[:, 0, :], scalar=EPS, in1=cl[:, 1, :], op0=ALU.add, op1=ALU.add)
-            s2 = prep.tile([P, SLOTS], F32)
-            nc.vector.tensor_tensor(out=s2[:], in0=s1[:], in1=cl[:, 2, :], op=ALU.add)
-            rs = prep.tile([P, SLOTS], F32)
-            nc.vector.reciprocal(out=rs[:], in_=s2[:])
-            nab = napool.tile([P, 2, SLOTS], F32)
-            nc.vector.scalar_tensor_tensor(
-                out=nab[:], in0=cl[:, 0:2, :], scalar=-63.0,
-                in1=rs[:].unsqueeze(1).to_broadcast([P, 2, SLOTS]), op0=ALU.mult, op1=ALU.mult)
-            na[b] = nab
+        def prepare(g):
+            b, gi = divmod(g, GPI)
+            if gi == 0 and b + 1 < IMAGES:
+                load(b + 1)
+            cl = prep.tile([P, 3, GS], BF16)
+            s1 = prep.tile([P, GS], F32)
+            s2 = prep.tile([P, GS], F32)
+            rs = prep.tile([P, GS], F32)
+            nag = napool.tile([P, GP, 2, 4], F32)
+            na[g] = nag
+            xs = xt[b][:, :, gi * GS:(gi + 1) * GS]
+            rsv = rs[:].rearrange("p (c j) -> p c j", j=4)
+            return [
+                lambda: nc.vector.tensor_scalar(out=cl[:], in0=xs, scalar1=0.0, scalar2=1.0, op0=ALU.max, op1=ALU.min),
+                lambda: nc.vector.scalar_tensor_tensor(out=s1[:], in0=cl[:, 0, :], scalar=EPS, in1=cl[:, 1, :],
+                                                       op0=ALU.add, op1=ALU.add),
+                lambda: nc.vector.tensor_tensor(out=s2[:], in0=s1[:], in1=cl[:, 2, :], op=ALU.add),
+                lambda: nc.vector.reciprocal(out=rs[:], in_=s2[:]),
+                lambda: nc.vector.scalar_tensor_tensor(out=nag[:, :, 0, :], in0=cl[:, 0, :].rearrange("p (c j) -> p c j", j=4),
+                                                       scalar=63.0, in1=rsv, op0=ALU.mult, op1=ALU.mult),
+                lambda: nc.vector.scalar_tensor_tensor(out=nag[:, :, 1, :], in0=cl[:, 1, :].rearrange("p (c j) -> p c j", j=4),
+                                                       scalar=63.0, in1=rsv, op0=ALU.mult, op1=ALU.mult),
+            ]
 
-        def shift(g, blk, j):
-            c, ch = divmod(blk, 2)
-            b, t = divmod(4 * (GP * g + c) + j, SLOTS)
-            return na[b][:, ch, t:t + 1]
-
-        def stage_a(g):
-            w = wpool.tile([P, 4, GCOLS], F32)
+        def squares(g, extra):
+            w = wpool.tile([P, BLKS, 4 * BINS], F32)
             wt[g] = w
-            na_blks = BLKS - NV
-            for blk in range(na_blks):
-                for j in range(4):
-                    nc.scalar.activation(out=w[:, j, blk * BINS:(blk + 1) * BINS], in_=jf[:], func=ACTF.Square,
-                                         bias=shift(g, blk, j), scale=1.0)
-            u = upool.tile([P, 4, NV * BINS], F32)
-            for k in range(NV):
-                for j in range(4):
-                    nc.vector.tensor_scalar(out=u[:, j, k * BINS:(k + 1) * BINS], in0=jf[:],
-                                            scalar1=shift(g, na_blks + k, j), scalar2=None, op0=ALU.add)
-            nc.vector.tensor_tensor(out=w[:, :, na_blks * BINS:], in0=u[:], in1=u[:], op=ALU.mult)
+            av = na[g][:].rearrange("p c h j -> p (c h) j")
+            for i in range(WA):
+                nc.scalar.activation(out=w[:, :, 4 * i:4 * i + 4], in_=av, func=ACTF.Square, bias=negj[:, i:i + 1], scale=1.0)
+            used = 0
+            for i in range(WA, BINS):
+                nc.vector.tensor_scalar(out=w[:, :, 4 * i:4 * i + 4], in0=av, scalar1=float(-i), scalar2=None, op0=ALU.add)
+                if used < len(extra) and (i - WA) % 3 == 2:
+                    extra[used]()
+                    used += 1
+            for f in extra[used:]:
+                f()
+
+        def vsquare(g):
+            reg = wt[g][:, :, 4 * WA:]
+            nc.vector.tensor_tensor(out=reg, in0=reg, in1=reg, op=ALU.mult)
 
         def stage_b(g):
-            q = qpool.tile([P, 4 * GCOLS], F32)
-            qt[g] = q
-            wv = wt[g][:].rearrange("p j n -> p n j")
-            nc.vector.scalar_tensor_tensor(out=q[:].rearrange("p (n j) -> p n j", j=4), in0=wv, scalar=2.0 * S2,
-                                           in1=wv, op0=ALU.add, op1=ALU.mult)
+            flat = wt[g][:].rearrange("p b e -> p (b e)")
+            nc.vector.scalar_tensor_tensor(out=flat, in0=flat, scalar=2.0 * S2, in1=flat, op0=ALU.add, op1=ALU.mult)
 
         def stage_c(g):
             k = kpool.tile([P, 4 * GCOLS], BF16, align_bytes=64)
             kt[g] = k
-            nc.scalar.activation(out=k[:], in_=qt[g][:], func=ACTF.Abs_reciprocal_sqrt, bias=one[:],
-                                 scale=1.0 / (S2 * S2))
+            nc.scalar.activation(out=k[:], in_=wt[g][:].rearrange("p b e -> p (b e)"), func=ACTF.Abs_reciprocal_sqrt,
+                                 bias=one[:], scale=1.0 / (S2 * S2))
 
         def finish(kb):
             hist = acc[kb][:].rearrange("p (i c) -> p i c", c=P)[:, :, BINS:P]
@@ -137,43 +142,42 @@ def tile_rgchromahistblock_kernel(tc, x, out):
         def stage_q(g):
             codes = cpool.tile([P, GCOLS], U32, align_bytes=64)
             scales = cpool.tile([P, GCOLS], U8, align_bytes=64)
-            nc.vector.quantize_mx(out=codes[:].bitcast(FP8X4), scales=scales[:], in_=kt[g][:])
-            done = []
+            lo = 0
+            for width in QW:
+                nc.vector.quantize_mx(out=codes[:, lo:lo + width].bitcast(FP8X4), scales=scales[:, lo:lo + width],
+                                      in_=kt[g][:, 4 * lo:4 * (lo + width)])
+                lo += width
+            b, gi = divmod(g, GPI)
             for c in range(GP):
-                b, cc = divmod(GP * g + c, PASSES)
                 cols = slice(c * P, (c + 1) * P)
                 nc.tensor.matmul_mx(
                     out=acc[b // 4][:, (b % 4) * P:(b % 4 + 1) * P],
                     lhsT=codes[:, cols].bitcast(FP8X4), lhsT_scale=scales[:, cols],
                     rhs=codes[:, cols].bitcast(FP8X4), rhs_scale=scales[:, cols],
-                    start=(cc == 0), stop=(cc == PASSES - 1))
-                if cc == PASSES - 1 and b % 4 == 3:
-                    done.append(b // 4)
-            return done
+                    start=(gi == 0 and c == 0), stop=(gi == GPI - 1 and c == GP - 1))
+            if gi == GPI - 1 and b % 4 == 3:
+                return [b // 4]
+            return []
 
-        first_group = [(b * SLOTS) // (4 * GP) for b in range(IMAGES)]
         load(0)
-        load(1)
-        load(2)
-        prepare(0)
-        prepared = 1
+        for g in range(2):
+            for f in prepare(g):
+                f()
         pending = []
         for n in range(-1, GROUPS + 2):
-            while prepared < IMAGES and first_group[prepared] <= n + 4:
-                if prepared + 2 < IMAGES:
-                    load(prepared + 2)
-                prepare(prepared)
-                prepared += 1
+            extra = prepare(n + 3) if n + 3 < GROUPS else []
             if n + 1 < GROUPS:
-                stage_a(n + 1)
-            if 0 <= n < GROUPS:
-                stage_b(n)
-            if 0 <= n - 1 < GROUPS:
-                stage_c(n - 1)
+                squares(n + 1, extra)
             for kb in pending:
                 finish(kb)
             pending = []
             if 0 <= n - 2:
                 pending = stage_q(n - 2)
+            if n + 1 < GROUPS:
+                vsquare(n + 1)
+            if 0 <= n < GROUPS:
+                stage_b(n)
+            if 0 <= n - 1 < GROUPS:
+                stage_c(n - 1)
         for kb in pending:
             finish(kb)

@@ -27,7 +27,7 @@ GS = 4 * GP
 BLKS = 2 * GP
 GCOLS = BLKS * BINS
 S2 = (63.0 * SIGMA) ** 2
-WA = 44
+WA = 48
 QW = (1024, 512, 256)
 
 FLOPS = 2 * IMAGES * PIXELS * BINS * BINS

@@ -19,16 +19,17 @@ BINS = 64
 EPS = 1e-6
 SIGMA = 0.02
 SLOTS = PIXELS // P
-PASSES = SLOTS // 4
-GP = 14
-GPI = PASSES // GP
-GROUPS = IMAGES * GPI
-GS = 4 * GP
-BLKS = 2 * GP
-GCOLS = BLKS * BINS
+HALVES = 2 * IMAGES
+HS = SLOTS // 2
+HP = HS // 4
+HB = 2 * HP
 S2 = (63.0 * SIGMA) ** 2
-WA = 48
-QW = (1024, 512, 256)
+SEQ = ((4, 2),) * 10 + ((2, 2),)
+NS = len(SEQ)
+START = [sum(na + nv for (na, nv) in SEQ[:i]) for i in range(NS)]
+assert START[-1] + sum(SEQ[-1]) == BINS
+assert NS >= 9
+QP = 8
 
 FLOPS = 2 * IMAGES * PIXELS * BINS * BINS
 
@@ -41,10 +42,10 @@ def tile_rgchromahistblock_kernel(tc, x, out):
         const = ctx.enter_context(tc.tile_pool(name="const", bufs=1))
         xin = ctx.enter_context(tc.tile_pool(name="xin", bufs=3))
         prep = ctx.enter_context(tc.tile_pool(name="prep", bufs=2))
-        napool = ctx.enter_context(tc.tile_pool(name="napool", bufs=6))
-        wpool = ctx.enter_context(tc.tile_pool(name="wpool", bufs=3))
-        kpool = ctx.enter_context(tc.tile_pool(name="kpool", bufs=3))
-        cpool = ctx.enter_context(tc.tile_pool(name="cpool", bufs=2))
+        napool = ctx.enter_context(tc.tile_pool(name="napool", bufs=4))
+        wpool = ctx.enter_context(tc.tile_pool(name="wpool", bufs=6))
+        kpool = ctx.enter_context(tc.tile_pool(name="kpool", bufs=2))
+        cpool = ctx.enter_context(tc.tile_pool(name="cpool", bufs=3))
         small = ctx.enter_context(tc.tile_pool(name="small", bufs=2))
         accp = ctx.enter_context(tc.psum_pool(name="accp", bufs=1))
         totp = ctx.enter_context(tc.psum_pool(name="totp", bufs=2))
@@ -65,63 +66,80 @@ def tile_rgchromahistblock_kernel(tc, x, out):
         na = {}
         wt = {}
         kt = {}
+        steps = {}
 
         def load(b):
             xb = xin.tile([P, 3, SLOTS], BF16)
             nc.sync.dma_start(out=xb[:], in_=xv[:, b])
             xt[b] = xb
 
-        def prepare(g):
-            b, gi = divmod(g, GPI)
-            if gi == 0 and b + 1 < IMAGES:
+        def prepare(h):
+            b, hi = divmod(h, 2)
+            if hi == 0 and b + 1 < IMAGES:
                 load(b + 1)
-            cl = prep.tile([P, 3, GS], BF16)
-            s1 = prep.tile([P, GS], F32)
-            s2 = prep.tile([P, GS], F32)
-            rs = prep.tile([P, GS], F32)
-            nag = napool.tile([P, GP, 2, 4], F32)
-            na[g] = nag
-            xs = xt[b][:, :, gi * GS:(gi + 1) * GS]
-            rsv = rs[:].rearrange("p (c j) -> p c j", j=4)
-            return [
-                lambda: nc.vector.tensor_scalar(out=cl[:], in0=xs, scalar1=0.0, scalar2=1.0, op0=ALU.max, op1=ALU.min),
-                lambda: nc.vector.scalar_tensor_tensor(out=s1[:], in0=cl[:, 0, :], scalar=EPS, in1=cl[:, 1, :],
-                                                       op0=ALU.add, op1=ALU.add),
-                lambda: nc.vector.tensor_tensor(out=s2[:], in0=s1[:], in1=cl[:, 2, :], op=ALU.add),
-                lambda: nc.vector.reciprocal(out=rs[:], in_=s2[:]),
-                lambda: nc.vector.scalar_tensor_tensor(out=nag[:, :, 0, :], in0=cl[:, 0, :].rearrange("p (c j) -> p c j", j=4),
-                                                       scalar=63.0, in1=rsv, op0=ALU.mult, op1=ALU.mult),
-                lambda: nc.vector.scalar_tensor_tensor(out=nag[:, :, 1, :], in0=cl[:, 1, :].rearrange("p (c j) -> p c j", j=4),
-                                                       scalar=63.0, in1=rsv, op0=ALU.mult, op1=ALU.mult),
-            ]
+            cl = prep.tile([P, 3, HS], BF16)
+            s1 = prep.tile([P, HS], F32)
+            s2 = prep.tile([P, HS], F32)
+            m = prep.tile([P, HS], F32)
+            y0 = prep.tile([P, HS], F32)
+            e = prep.tile([P, HS], F32)
+            yn = prep.tile([P, HS], F32)
+            nah = napool.tile([P, HP, 2, 4], F32)
+            na[h] = nah
+            xs = xt[b][:, :, hi * HS:(hi + 1) * HS]
+            ynv = yn[:].rearrange("p (c j) -> p c j", j=4)
+            steps[h] = {
+                0: lambda: nc.vector.tensor_scalar(out=cl[:], in0=xs, scalar1=0.0, scalar2=1.0, op0=ALU.max, op1=ALU.min),
+                1: lambda: nc.vector.scalar_tensor_tensor(out=s1[:], in0=cl[:, 0, :], scalar=EPS, in1=cl[:, 1, :],
+                                                          op0=ALU.add, op1=ALU.add),
+                2: lambda: nc.vector.tensor_tensor(out=s2[:], in0=s1[:], in1=cl[:, 2, :], op=ALU.add),
+                4: lambda: nc.scalar.activation(out=m[:], in_=s2[:], func=ACTF.Abs_reciprocal_sqrt, scale=1.0),
+                6: lambda: nc.vector.tensor_tensor(out=y0[:], in0=m[:], in1=m[:], op=ALU.mult),
+                7: lambda: nc.vector.tensor_tensor(out=e[:], in0=s2[:], in1=y0[:], op=ALU.mult),
+                8: lambda: nc.vector.scalar_tensor_tensor(out=yn[:], in0=e[:], scalar=2.0, in1=y0[:],
+                                                          op0=ALU.subtract, op1=ALU.mult),
+                NS: lambda: nc.vector.scalar_tensor_tensor(
+                    out=nah[:, :, 0, :], in0=cl[:, 0, :].rearrange("p (c j) -> p c j", j=4), scalar=126.0, in1=ynv,
+                    op0=ALU.mult, op1=ALU.mult),
+                NS + 1: lambda: nc.vector.scalar_tensor_tensor(
+                    out=nah[:, :, 1, :], in0=cl[:, 1, :].rearrange("p (c j) -> p c j", j=4), scalar=126.0, in1=ynv,
+                    op0=ALU.mult, op1=ALU.mult),
+            }
 
-        def squares(g, extra):
-            w = wpool.tile([P, BLKS, 4 * BINS], F32)
-            wt[g] = w
-            av = na[g][:].rearrange("p c h j -> p (c h) j")
-            for i in range(WA):
-                nc.scalar.activation(out=w[:, :, 4 * i:4 * i + 4], in_=av, func=ACTF.Square, bias=negj[:, i:i + 1], scale=1.0)
-            used = 0
-            for i in range(WA, BINS):
-                nc.vector.tensor_scalar(out=w[:, :, 4 * i:4 * i + 4], in0=av, scalar1=float(-i), scalar2=None, op0=ALU.add)
-                if used < len(extra) and (i - WA) % 3 == 2:
-                    extra[used]()
-                    used += 1
-            for f in extra[used:]:
-                f()
+        def prep_step(h, k):
+            if h < HALVES and k in steps[h]:
+                steps[h][k]()
 
-        def vsquare(g):
-            reg = wt[g][:, :, 4 * WA:]
-            nc.vector.tensor_tensor(out=reg, in0=reg, in1=reg, op=ALU.mult)
+        def squares(i):
+            h, si = divmod(i, NS)
+            w = wpool.tile([P, HB, 4 * sum(SEQ[si])], F32)
+            wt[i] = w
+            dv = na[h][:].rearrange("p c h j -> p (c h) j")
+            for k in range(SEQ[si][0]):
+                nc.scalar.activation(out=w[:, :, 4 * k:4 * k + 4], in_=dv, func=ACTF.Square,
+                                     bias=negj[:, START[si] + k:START[si] + k + 1], scale=-0.5)
 
-        def stage_b(g):
-            flat = wt[g][:].rearrange("p b e -> p (b e)")
+        def derive(i, part):
+            h, si = divmod(i, NS)
+            n_sc, n_ve = SEQ[si]
+            w = wt[i]
+            dv = na[h][:].rearrange("p c h j -> p (c h) j")
+            cut = n_sc + (n_ve + 1) // 2
+            for k in (range(n_sc, cut) if part == 0 else range(cut, n_sc + n_ve)):
+                nc.vector.scalar_tensor_tensor(out=w[:, :, 4 * k:4 * k + 4], in0=dv, scalar=float(2 * (START[si] + k) - 1),
+                                               in1=w[:, :, 4 * k - 4:4 * k], op0=ALU.add, op1=ALU.add)
+
+        def stage_b(i):
+            flat = wt[i][:].rearrange("p b e -> p (b e)")
             nc.vector.scalar_tensor_tensor(out=flat, in0=flat, scalar=2.0 * S2, in1=flat, op0=ALU.add, op1=ALU.mult)
 
-        def stage_c(g):
-            k = kpool.tile([P, 4 * GCOLS], BF16, align_bytes=64)
-            kt[g] = k
-            nc.scalar.activation(out=k[:], in_=wt[g][:].rearrange("p b e -> p (b e)"), func=ACTF.Abs_reciprocal_sqrt,
+        def stage_c(i):
+            h, si = divmod(i, NS)
+            if si == 0:
+                kh = kpool.tile([P, HB, 4 * BINS], BF16, align_bytes=64)
+                kt[h] = kh
+            lo = 4 * START[si]
+            nc.scalar.activation(out=kt[h][:, :, lo:lo + 4 * sum(SEQ[si])], in_=wt[i][:], func=ACTF.Abs_reciprocal_sqrt,
                                  bias=one[:], scale=1.0 / (S2 * S2))
 
         def finish(kb):
@@ -139,45 +157,65 @@ def tile_rgchromahistblock_kernel(tc, x, out):
                                     op=ALU.mult)
             nc.sync.dma_start(out=outv[:, 4 * kb:4 * kb + 4, :], in_=o[:])
 
-        def stage_q(g):
-            codes = cpool.tile([P, GCOLS], U32, align_bytes=64)
-            scales = cpool.tile([P, GCOLS], U8, align_bytes=64)
-            lo = 0
-            for width in QW:
-                nc.vector.quantize_mx(out=codes[:, lo:lo + width].bitcast(FP8X4), scales=scales[:, lo:lo + width],
-                                      in_=kt[g][:, 4 * lo:4 * (lo + width)])
-                lo += width
-            b, gi = divmod(g, GPI)
-            for c in range(GP):
+        def quantise(h, first):
+            n = min(QP, HP - first)
+            codes = cpool.tile([P, QP * P], U32, align_bytes=64)
+            scales = cpool.tile([P, QP * P], U8, align_bytes=64)
+            kflat = kt[h][:].rearrange("p b e -> p (b e)")
+            nc.vector.quantize_mx(out=codes[:, 0:n * P].bitcast(FP8X4), scales=scales[:, 0:n * P],
+                                  in_=kflat[:, first * 4 * P:(first + n) * 4 * P])
+            b, hi = divmod(h, 2)
+            for c in range(n):
                 cols = slice(c * P, (c + 1) * P)
                 nc.tensor.matmul_mx(
                     out=acc[b // 4][:, (b % 4) * P:(b % 4 + 1) * P],
                     lhsT=codes[:, cols].bitcast(FP8X4), lhsT_scale=scales[:, cols],
                     rhs=codes[:, cols].bitcast(FP8X4), rhs_scale=scales[:, cols],
-                    start=(gi == 0 and c == 0), stop=(gi == GPI - 1 and c == GP - 1))
-            if gi == GPI - 1 and b % 4 == 3:
+                    start=(hi == 0 and first + c == 0), stop=(hi == 1 and first + c == HP - 1))
+            if hi == 1 and first + n == HP and b % 4 == 3:
                 return [b // 4]
             return []
 
         load(0)
-        for g in range(2):
-            for f in prepare(g):
-                f()
+        for h in range(2):
+            prepare(h)
+            for k in range(NS + 2):
+                prep_step(h, k)
+        total = HALVES * NS
+        calls = []
         pending = []
-        for n in range(-1, GROUPS + 2):
-            extra = prepare(n + 3) if n + 3 < GROUPS else []
-            if n + 1 < GROUPS:
-                squares(n + 1, extra)
+        squares(0)
+        squares(1)
+        derive(0, 0)
+        derive(0, 1)
+        for i in range(total + 1):
+            h, si = divmod(i, NS)
+            if si == 0 and h + 2 < HALVES:
+                prepare(h + 2)
+            if i + 2 < total:
+                squares(i + 2)
+            if i + 1 < total:
+                derive(i + 1, 0)
             for kb in pending:
                 finish(kb)
             pending = []
-            if 0 <= n - 2:
-                pending = stage_q(n - 2)
-            if n + 1 < GROUPS:
-                vsquare(n + 1)
-            if 0 <= n < GROUPS:
-                stage_b(n)
-            if 0 <= n - 1 < GROUPS:
-                stage_c(n - 1)
+            if calls:
+                pending = quantise(calls[0][0], calls[0][1])
+                calls = calls[1:]
+            if h >= 1:
+                prep_step(h + 1, NS + si)
+            prep_step(h + 2, si)
+            if i < total:
+                stage_b(i)
+            if i + 1 < total:
+                derive(i + 1, 1)
+            if i >= 1:
+                stage_c(i - 1)
+                if (i - 1) % NS == NS - 1:
+                    calls = calls + [((i - 1) // NS, first) for first in range(0, HP, QP)]
+        for (h, first) in calls:
+            for kb in pending:
+                finish(kb)
+            pending = quantise(h, first)
         for kb in pending:
             finish(kb)

@@ -1,6 +1,7 @@
 from contextlib import ExitStack
 
 import concourse.mybir as mybir
+from concourse.masks import make_identity
 
 F32 = mybir.dt.float32
 BF16 = mybir.dt.bfloat16
@@ -24,12 +25,14 @@ HS = SLOTS // 2
 HP = HS // 4
 HB = 2 * HP
 S2 = (63.0 * SIGMA) ** 2
-SEQ = ((4, 2),) * 10 + ((2, 2),)
-NS = len(SEQ)
-START = [sum(na + nv for (na, nv) in SEQ[:i]) for i in range(NS)]
-assert START[-1] + sum(SEQ[-1]) == BINS
-assert NS >= 9
+NB = 8
+SL = BINS // NB
+TOTAL = HALVES * SL
+GROUP = 3
+NG = (TOTAL + GROUP - 1) // GROUP
+RB = 77
 QP = 8
+QMAX = 3
 
 FLOPS = 2 * IMAGES * PIXELS * BINS * BINS
 
@@ -43,16 +46,19 @@ def tile_rgchromahistblock_kernel(tc, x, out):
         xin = ctx.enter_context(tc.tile_pool(name="xin", bufs=3))
         prep = ctx.enter_context(tc.tile_pool(name="prep", bufs=2))
         napool = ctx.enter_context(tc.tile_pool(name="napool", bufs=4))
-        wpool = ctx.enter_context(tc.tile_pool(name="wpool", bufs=6))
+        wpool = ctx.enter_context(tc.tile_pool(name="wpool", bufs=2 * GROUP))
         kpool = ctx.enter_context(tc.tile_pool(name="kpool", bufs=2))
         cpool = ctx.enter_context(tc.tile_pool(name="cpool", bufs=3))
         small = ctx.enter_context(tc.tile_pool(name="small", bufs=2))
         accp = ctx.enter_context(tc.psum_pool(name="accp", bufs=1))
+        d4pool = ctx.enter_context(tc.psum_pool(name="d4pool", bufs=2))
         totp = ctx.enter_context(tc.psum_pool(name="totp", bufs=2))
         ctx.enter_context(tc.manual_schedule())
 
         ji = const.tile([P, BINS], I32)
         nc.gpsimd.iota(out=ji[:], pattern=[[1, BINS]], base=0, channel_multiplier=0)
+        ident = const.tile([P, P], F32)
+        make_identity(nc, ident[:])
         negj = const.tile([P, BINS], F32)
         nc.vector.tensor_scalar(out=negj[:], in0=ji[:], scalar1=-1.0, scalar2=None, op0=ALU.mult)
         one = const.tile([P, 1], F32)
@@ -64,9 +70,10 @@ def tile_rgchromahistblock_kernel(tc, x, out):
 
         xt = {}
         na = {}
+        d4 = {}
         wt = {}
         kt = {}
-        steps = {}
+        stages = {}
 
         def load(b):
             xb = xin.tile([P, 3, SLOTS], BF16)
@@ -84,63 +91,104 @@ def tile_rgchromahistblock_kernel(tc, x, out):
             y0 = prep.tile([P, HS], F32)
             e = prep.tile([P, HS], F32)
             yn = prep.tile([P, HS], F32)
-            nah = napool.tile([P, HP, 2, 4], F32)
-            na[h] = nah
             xs = xt[b][:, :, hi * HS:(hi + 1) * HS]
             ynv = yn[:].rearrange("p (c j) -> p c j", j=4)
-            steps[h] = {
-                0: lambda: nc.vector.tensor_scalar(out=cl[:], in0=xs, scalar1=0.0, scalar2=1.0, op0=ALU.max, op1=ALU.min),
-                1: lambda: nc.vector.scalar_tensor_tensor(out=s1[:], in0=cl[:, 0, :], scalar=EPS, in1=cl[:, 1, :],
-                                                          op0=ALU.add, op1=ALU.add),
-                2: lambda: nc.vector.tensor_tensor(out=s2[:], in0=s1[:], in1=cl[:, 2, :], op=ALU.add),
-                4: lambda: nc.scalar.activation(out=m[:], in_=s2[:], func=ACTF.Abs_reciprocal_sqrt, scale=1.0),
-                6: lambda: nc.vector.tensor_tensor(out=y0[:], in0=m[:], in1=m[:], op=ALU.mult),
-                7: lambda: nc.vector.tensor_tensor(out=e[:], in0=s2[:], in1=y0[:], op=ALU.mult),
-                8: lambda: nc.vector.scalar_tensor_tensor(out=yn[:], in0=e[:], scalar=2.0, in1=y0[:],
-                                                          op0=ALU.subtract, op1=ALU.mult),
-                NS: lambda: nc.vector.scalar_tensor_tensor(
-                    out=nah[:, :, 0, :], in0=cl[:, 0, :].rearrange("p (c j) -> p c j", j=4), scalar=126.0, in1=ynv,
-                    op0=ALU.mult, op1=ALU.mult),
-                NS + 1: lambda: nc.vector.scalar_tensor_tensor(
-                    out=nah[:, :, 1, :], in0=cl[:, 1, :].rearrange("p (c j) -> p c j", j=4), scalar=126.0, in1=ynv,
-                    op0=ALU.mult, op1=ALU.mult),
-            }
 
-        def prep_step(h, k):
-            if h < HALVES and k in steps[h]:
-                steps[h][k]()
+            def chroma(ch):
+                if ch == 0:
+                    nah = napool.tile([P, HP, 2, 4], F32)
+                    na[h] = nah
+                nc.vector.scalar_tensor_tensor(
+                    out=na[h][:, :, ch, :], in0=cl[:, ch, :].rearrange("p (c j) -> p c j", j=4), scalar=252.0, in1=ynv,
+                    op0=ALU.mult, op1=ALU.mult)
 
-        def squares(i):
-            h, si = divmod(i, NS)
-            w = wpool.tile([P, HB, 4 * sum(SEQ[si])], F32)
+            def to_psum():
+                dp = d4pool.tile([P, 512], F32)
+                d4[h] = dp
+                nc.tensor.matmul(out=dp[:, 0:2 * HS], lhsT=ident[:], rhs=na[h][:].rearrange("p c h j -> p (c h j)"),
+                                 start=True, stop=True)
+
+            stages[h] = [
+                [
+                    lambda: nc.vector.tensor_scalar(out=cl[:], in0=xs, scalar1=0.0, scalar2=1.0, op0=ALU.max, op1=ALU.min),
+                    lambda: nc.vector.scalar_tensor_tensor(out=s1[:], in0=cl[:, 0, :], scalar=EPS, in1=cl[:, 1, :],
+                                                           op0=ALU.add, op1=ALU.add),
+                    lambda: nc.vector.tensor_tensor(out=s2[:], in0=s1[:], in1=cl[:, 2, :], op=ALU.add),
+                    lambda: nc.scalar.activation(out=m[:], in_=s2[:], func=ACTF.Abs_reciprocal_sqrt, scale=1.0),
+                ],
+                [
+                    lambda: nc.vector.tensor_tensor(out=y0[:], in0=m[:], in1=m[:], op=ALU.mult),
+                    lambda: nc.vector.tensor_tensor(out=e[:], in0=s2[:], in1=y0[:], op=ALU.mult),
+                    lambda: nc.vector.scalar_tensor_tensor(out=yn[:], in0=e[:], scalar=2.0, in1=y0[:],
+                                                           op0=ALU.subtract, op1=ALU.mult),
+                    lambda: chroma(0),
+                ],
+                [
+                    lambda: chroma(1),
+                    to_psum,
+                ],
+            ]
+
+        def seeds(i):
+            h, si = divmod(i, SL)
+            w = wpool.tile([P, HB, 4 * NB], F32)
             wt[i] = w
             dv = na[h][:].rearrange("p c h j -> p (c h) j")
-            for k in range(SEQ[si][0]):
+            for k in range(2):
                 nc.scalar.activation(out=w[:, :, 4 * k:4 * k + 4], in_=dv, func=ACTF.Square,
-                                     bias=negj[:, START[si] + k:START[si] + k + 1], scale=-0.5)
+                                     bias=negj[:, NB * si + k:NB * si + k + 1], scale=-0.25)
 
-        def derive(i, part):
-            h, si = divmod(i, NS)
-            n_sc, n_ve = SEQ[si]
+        def derive(i, k):
+            h, si = divmod(i, SL)
             w = wt[i]
-            dv = na[h][:].rearrange("p c h j -> p (c h) j")
-            cut = n_sc + (n_ve + 1) // 2
-            for k in (range(n_sc, cut) if part == 0 else range(cut, n_sc + n_ve)):
-                nc.vector.scalar_tensor_tensor(out=w[:, :, 4 * k:4 * k + 4], in0=dv, scalar=float(2 * (START[si] + k) - 1),
-                                               in1=w[:, :, 4 * k - 4:4 * k], op0=ALU.add, op1=ALU.add)
+            dv = d4[h][:, 0:2 * HS].rearrange("p (b j) -> p b j", j=4)
+            nc.vector.scalar_tensor_tensor(out=w[:, :, 4 * k:4 * k + 4], in0=dv, scalar=float(4 * (NB * si + k) - 4),
+                                           in1=w[:, :, 4 * k - 8:4 * k - 4], op0=ALU.add, op1=ALU.add)
 
-        def stage_b(i):
-            flat = wt[i][:].rearrange("p b e -> p (b e)")
-            nc.vector.scalar_tensor_tensor(out=flat, in0=flat, scalar=2.0 * S2, in1=flat, op0=ALU.add, op1=ALU.mult)
+        def derive_group(g):
+            for step in range(3):
+                for i in g[0:2]:
+                    for par in range(2):
+                        derive(i, 2 + 2 * step + par)
+            for i in g[2:3]:
+                for step in range(3):
+                    for par in range(2):
+                        derive(i, 2 + 2 * step + par)
 
-        def stage_c(i):
-            h, si = divmod(i, NS)
-            if si == 0:
+        def rows(i, r0, r1):
+            return wt[i][:, r0:r1, :].rearrange("p b e -> p (b e)")
+
+        def second(eng, i, r0, r1):
+            flat = rows(i, r0, r1)
+            eng.scalar_tensor_tensor(out=flat, in0=flat, scalar=2.0 * S2, in1=flat, op0=ALU.add, op1=ALU.mult)
+
+        def second_scalar(i, r0, r1):
+            flat = rows(i, r0, r1)
+            nc.scalar.activation(out=flat, in_=flat, func=ACTF.Square, bias=one[:], scale=1.0 / S2)
+
+        def kernel_values(i):
+            h, si = divmod(i, SL)
+            if h not in kt:
                 kh = kpool.tile([P, HB, 4 * BINS], BF16, align_bytes=64)
                 kt[h] = kh
-            lo = 4 * START[si]
-            nc.scalar.activation(out=kt[h][:, :, lo:lo + 4 * sum(SEQ[si])], in_=wt[i][:], func=ACTF.Abs_reciprocal_sqrt,
-                                 bias=one[:], scale=1.0 / (S2 * S2))
+            return kt[h][:, :, 4 * NB * si:4 * NB * (si + 1)]
+
+        def root(i):
+            flat = rows(i, 0, HB)
+            nc.scalar.activation(out=flat, in_=flat, func=ACTF.Abs_reciprocal_sqrt, bias=one[:], scale=1.0 / S2)
+
+        def root_squared(i):
+            dst = kernel_values(i)
+            nc.vector.memset(dst[:, 0, 0:16], 0.0)
+            nc.gpsimd.tensor_tensor(out=dst, in0=wt[i][:], in1=wt[i][:], op=ALU.mult)
+
+        def third(i, r0, r1, squared_by_scalar):
+            dst = kernel_values(i)[:, r0:r1, :]
+            if squared_by_scalar:
+                nc.scalar.activation(out=dst, in_=wt[i][:, r0:r1, :], func=ACTF.Abs_reciprocal_sqrt, scale=1.0)
+            else:
+                nc.scalar.activation(out=dst, in_=wt[i][:, r0:r1, :], func=ACTF.Abs_reciprocal_sqrt,
+                                     bias=one[:], scale=1.0 / (S2 * S2))
 
         def finish(kb):
             hist = acc[kb][:].rearrange("p (i c) -> p i c", c=P)[:, :, BINS:P]
@@ -176,43 +224,86 @@ def tile_rgchromahistblock_kernel(tc, x, out):
                 return [b // 4]
             return []
 
+        groups = [list(range(g, min(g + GROUP, TOTAL))) for g in range(0, TOTAL, GROUP)]
+
+        def on_gpsimd(n):
+            return 0 <= n and n + 1 < NG and len(groups[n]) == GROUP and len(groups[n + 1]) == GROUP
+
+        plan = {}
+        for h in range(2, HALVES):
+            for s in range(3):
+                c = (SL * (h - 2)) // GROUP + 1 + s
+                plan[c] = plan.get(c, []) + [(h, s)]
+
         load(0)
         for h in range(2):
             prepare(h)
-            for k in range(NS + 2):
-                prep_step(h, k)
-        total = HALVES * NS
+            for st in stages[h]:
+                for f in st:
+                    f()
+        for i in groups[0]:
+            seeds(i)
+
         calls = []
         pending = []
-        squares(0)
-        squares(1)
-        derive(0, 0)
-        derive(0, 1)
-        for i in range(total + 1):
-            h, si = divmod(i, NS)
-            if si == 0 and h + 2 < HALVES:
-                prepare(h + 2)
-            if i + 2 < total:
-                squares(i + 2)
-            if i + 1 < total:
-                derive(i + 1, 0)
-            for kb in pending:
-                finish(kb)
+        for n in range(NG + 1):
+            prev = groups[n - 1] if n >= 1 else []
+            cur = groups[n] if n < NG else []
+            nxt = groups[n + 1] if n + 1 < NG else []
+            if len(prev) >= 2:
+                second_scalar(prev[1], 0, RB)
+            if len(prev) >= 1:
+                third(prev[0], 0, HB, False)
+            if len(nxt) >= 1:
+                seeds(nxt[0])
+            if on_gpsimd(n - 1):
+                root_squared(prev[2])
+            derive_group(cur)
+            if len(prev) >= 2:
+                third(prev[1], 0, RB, True)
+                third(prev[1], RB, HB, False)
+            if len(nxt) >= 2:
+                seeds(nxt[1])
+            if len(prev) >= 3 and not on_gpsimd(n - 1):
+                third(prev[2], 0, HB, False)
+            if on_gpsimd(n):
+                root(cur[2])
+            if len(nxt) >= 3:
+                seeds(nxt[2])
+            for i in prev:
+                if i % SL == SL - 1:
+                    calls = calls + [(i // SL, first) for first in range(0, HP, QP)]
+            big = []
+            if len(cur) >= 1:
+                big.append(lambda: second(nc.vector, cur[0], 0, HB))
+            if len(cur) >= 2:
+                big.append(lambda: second(nc.vector, cur[1], RB, HB))
+            if len(cur) >= 3 and not on_gpsimd(n):
+                big.append(lambda: second(nc.vector, cur[2], 0, HB))
+            little = []
+            for (h, s) in plan.get(n, []):
+                if s == 0:
+                    prepare(h)
+                little.extend(stages[h][s])
+            done = pending
             pending = []
-            if calls:
-                pending = quantise(calls[0][0], calls[0][1])
-                calls = calls[1:]
-            if h >= 1:
-                prep_step(h + 1, NS + si)
-            prep_step(h + 2, si)
-            if i < total:
-                stage_b(i)
-            if i + 1 < total:
-                derive(i + 1, 1)
-            if i >= 1:
-                stage_c(i - 1)
-                if (i - 1) % NS == NS - 1:
-                    calls = calls + [((i - 1) // NS, first) for first in range(0, HP, QP)]
+            take = calls[0:QMAX]
+            calls = calls[QMAX:]
+            used = 0
+            for f in big:
+                f()
+                if used < len(little):
+                    little[used]()
+                    used += 1
+            for kb in done:
+                finish(kb)
+            for (h, first) in take:
+                pending = pending + quantise(h, first)
+                if used < len(little):
+                    little[used]()
+                    used += 1
+            for f in little[used:]:
+                f()
         for (h, first) in calls:
             for kb in pending:
                 finish(kb)

@@ -146,14 +146,9 @@ def tile_rgchromahistblock_kernel(tc, x, out):
                                            in1=w[:, :, 4 * k - 8:4 * k - 4], op0=ALU.add, op1=ALU.add)
 
         def derive_group(g):
-            for step in range(3):
-                for i in g[0:2]:
-                    for par in range(2):
-                        derive(i, 2 + 2 * step + par)
-            for i in g[2:3]:
-                for step in range(3):
-                    for par in range(2):
-                        derive(i, 2 + 2 * step + par)
+            for i in g:
+                for k in range(2, NB):
+                    derive(i, k)
 
         def rows(i, r0, r1):
             return wt[i][:, r0:r1, :].rearrange("p b e -> p (b e)")
@@ -252,22 +247,20 @@ def tile_rgchromahistblock_kernel(tc, x, out):
             nxt = groups[n + 1] if n + 1 < NG else []
             if len(prev) >= 2:
                 second_scalar(prev[1], 0, RB)
+                third(prev[1], RB, HB, False)
             if len(prev) >= 1:
                 third(prev[0], 0, HB, False)
-            if len(nxt) >= 1:
-                seeds(nxt[0])
-            if on_gpsimd(n - 1):
-                root_squared(prev[2])
-            derive_group(cur)
             if len(prev) >= 2:
                 third(prev[1], 0, RB, True)
-                third(prev[1], RB, HB, False)
-            if len(nxt) >= 2:
-                seeds(nxt[1])
             if len(prev) >= 3 and not on_gpsimd(n - 1):
                 third(prev[2], 0, HB, False)
+            if len(nxt) >= 1:
+                seeds(nxt[0])
+            derive_group(cur)
             if on_gpsimd(n):
                 root(cur[2])
+            if len(nxt) >= 2:
+                seeds(nxt[1])
             if len(nxt) >= 3:
                 seeds(nxt[2])
             for i in prev:
@@ -276,8 +269,6 @@ def tile_rgchromahistblock_kernel(tc, x, out):
             big = []
             if len(cur) >= 1:
                 big.append(lambda: second(nc.vector, cur[0], 0, HB))
-            if len(cur) >= 2:
-                big.append(lambda: second(nc.vector, cur[1], RB, HB))
             if len(cur) >= 3 and not on_gpsimd(n):
                 big.append(lambda: second(nc.vector, cur[2], 0, HB))
             little = []
@@ -304,6 +295,10 @@ def tile_rgchromahistblock_kernel(tc, x, out):
                     used += 1
             for f in little[used:]:
                 f()
+            if on_gpsimd(n):
+                root_squared(cur[2])
+            if len(cur) >= 2:
+                second(nc.vector, cur[1], RB, HB)
         for (h, first) in calls:
             for kb in pending:
                 finish(kb)

@@ -29,10 +29,14 @@ NB = 8
 SL = BINS // NB
 TOTAL = HALVES * SL
 GROUP = 3
-NG = (TOTAL + GROUP - 1) // GROUP
-RB = 77
-QP = 8
-QMAX = 3
+NFULL = TOTAL // GROUP - 1
+CUT = 48
+AB = 11
+PB_LONG = 24
+PB_SHORT = 12
+LAST = 20
+QP = 4
+QCALLS = (HP + QP - 1) // QP
 
 FLOPS = 2 * IMAGES * PIXELS * BINS * BINS
 
@@ -46,9 +50,9 @@ def tile_rgchromahistblock_kernel(tc, x, out):
         xin = ctx.enter_context(tc.tile_pool(name="xin", bufs=3))
         prep = ctx.enter_context(tc.tile_pool(name="prep", bufs=2))
         napool = ctx.enter_context(tc.tile_pool(name="napool", bufs=4))
-        wpool = ctx.enter_context(tc.tile_pool(name="wpool", bufs=2 * GROUP))
+        wpool = ctx.enter_context(tc.tile_pool(name="wpool", bufs=2))
         kpool = ctx.enter_context(tc.tile_pool(name="kpool", bufs=2))
-        cpool = ctx.enter_context(tc.tile_pool(name="cpool", bufs=3))
+        cpool = ctx.enter_context(tc.tile_pool(name="cpool", bufs=4))
         small = ctx.enter_context(tc.tile_pool(name="small", bufs=2))
         accp = ctx.enter_context(tc.psum_pool(name="accp", bufs=1))
         d4pool = ctx.enter_context(tc.psum_pool(name="d4pool", bufs=2))
@@ -129,26 +133,44 @@ def tile_rgchromahistblock_kernel(tc, x, out):
                 ],
             ]
 
+        def squares_tile(i):
+            if i not in wt:
+                w = wpool.tile([P, HB, 4 * NB], F32, tag="w%d" % (i % GROUP))
+                wt[i] = w
+            return wt[i]
+
+        def squared(i):
+            if i in (1, 2):
+                return NB
+            if (i % GROUP == 0 and i <= GROUP * NFULL) or i % SL == 0:
+                return 2
+            return 0
+
         def seeds(i):
+            if squared(i) == 0:
+                return
             h, si = divmod(i, SL)
-            w = wpool.tile([P, HB, 4 * NB], F32)
-            wt[i] = w
+            w = squares_tile(i)
             dv = na[h][:].rearrange("p c h j -> p (c h) j")
-            for k in range(2):
+            for k in range(squared(i)):
                 nc.scalar.activation(out=w[:, :, 4 * k:4 * k + 4], in_=dv, func=ACTF.Square,
                                      bias=negj[:, NB * si + k:NB * si + k + 1], scale=-0.25)
 
         def derive(i, k):
             h, si = divmod(i, SL)
-            w = wt[i]
+            w = squares_tile(i)
+            before = w[:, :, 4 * k - 8:4 * k - 4] if k >= 2 else wt[i - 1][:, :, 4 * (NB + k) - 8:4 * (NB + k) - 4]
             dv = d4[h][:, 0:2 * HS].rearrange("p (b j) -> p b j", j=4)
             nc.vector.scalar_tensor_tensor(out=w[:, :, 4 * k:4 * k + 4], in0=dv, scalar=float(4 * (NB * si + k) - 4),
-                                           in1=w[:, :, 4 * k - 8:4 * k - 4], op0=ALU.add, op1=ALU.add)
+                                           in1=before, op0=ALU.add, op1=ALU.add)
 
         def derive_group(g):
             for i in g:
-                for k in range(2, NB):
+                for k in range(squared(i), NB):
                     derive(i, k)
+
+        def derivations(g):
+            return sum(NB - squared(i) for i in g)
 
         def rows(i, r0, r1):
             return wt[i][:, r0:r1, :].rearrange("p b e -> p (b e)")
@@ -168,14 +190,15 @@ def tile_rgchromahistblock_kernel(tc, x, out):
                 kt[h] = kh
             return kt[h][:, :, 4 * NB * si:4 * NB * (si + 1)]
 
-        def root(i):
-            flat = rows(i, 0, HB)
+        def root(i, r1):
+            flat = rows(i, 0, r1)
             nc.scalar.activation(out=flat, in_=flat, func=ACTF.Abs_reciprocal_sqrt, bias=one[:], scale=1.0 / S2)
 
-        def root_squared(i):
-            dst = kernel_values(i)
-            nc.vector.memset(dst[:, 0, 0:16], 0.0)
-            nc.gpsimd.tensor_tensor(out=dst, in0=wt[i][:], in1=wt[i][:], op=ALU.mult)
+        def root_squared(i, r1, hold):
+            dst = kernel_values(i)[:, 0:r1, :]
+            if hold:
+                nc.vector.memset(dst[:, 0, 0:16], 0.0)
+            nc.gpsimd.tensor_tensor(out=dst, in0=wt[i][:, 0:r1, :], in1=wt[i][:, 0:r1, :], op=ALU.mult)
 
         def third(i, r0, r1, squared_by_scalar):
             dst = kernel_values(i)[:, r0:r1, :]
@@ -204,9 +227,8 @@ def tile_rgchromahistblock_kernel(tc, x, out):
             n = min(QP, HP - first)
             codes = cpool.tile([P, QP * P], U32, align_bytes=64)
             scales = cpool.tile([P, QP * P], U8, align_bytes=64)
-            kflat = kt[h][:].rearrange("p b e -> p (b e)")
             nc.vector.quantize_mx(out=codes[:, 0:n * P].bitcast(FP8X4), scales=scales[:, 0:n * P],
-                                  in_=kflat[:, first * 4 * P:(first + n) * 4 * P])
+                                  in_=kt[h][:, 2 * first:2 * (first + n), :].rearrange("p b e -> p (b e)"))
             b, hi = divmod(h, 2)
             for c in range(n):
                 cols = slice(c * P, (c + 1) * P)
@@ -219,58 +241,49 @@ def tile_rgchromahistblock_kernel(tc, x, out):
                 return [b // 4]
             return []
 
-        groups = [list(range(g, min(g + GROUP, TOTAL))) for g in range(0, TOTAL, GROUP)]
+        groups = [list(range(GROUP * n, GROUP * n + GROUP)) for n in range(NFULL)] + [list(range(GROUP * NFULL, TOTAL))]
 
-        def on_gpsimd(n):
-            return 0 <= n and n + 1 < NG and len(groups[n]) == GROUP and len(groups[n + 1]) == GROUP
+        def gpsimd_blocks(n):
+            return PB_LONG if derivations(groups[n + 1]) >= GROUP * NB - 2 else PB_SHORT
 
-        plan = {}
+        def calls_of(h):
+            return [(h, first) for first in range(0, HP, QP)]
+
+        plan = {0: [(1, 1), (1, 2)]}
         for h in range(2, HALVES):
             for s in range(3):
                 c = (SL * (h - 2)) // GROUP + 1 + s
                 plan[c] = plan.get(c, []) + [(h, s)]
 
         load(0)
-        for h in range(2):
-            prepare(h)
-            for st in stages[h]:
-                for f in st:
-                    f()
+        prepare(0)
+        prepare(1)
+        for st in (stages[0][0], stages[1][0], stages[0][1], stages[0][2]):
+            for f in st:
+                f()
         for i in groups[0]:
             seeds(i)
 
         calls = []
         pending = []
-        for n in range(NG + 1):
+        credit = 0
+        for n in range(NFULL):
+            cur = groups[n]
             prev = groups[n - 1] if n >= 1 else []
-            cur = groups[n] if n < NG else []
-            nxt = groups[n + 1] if n + 1 < NG else []
-            if len(prev) >= 2:
-                second_scalar(prev[1], 0, RB)
-                third(prev[1], RB, HB, False)
-            if len(prev) >= 1:
-                third(prev[0], 0, HB, False)
-            if len(prev) >= 2:
-                third(prev[1], 0, RB, True)
-            if len(prev) >= 3 and not on_gpsimd(n - 1):
-                third(prev[2], 0, HB, False)
-            if len(nxt) >= 1:
-                seeds(nxt[0])
+            nxt = groups[n + 1]
+            pb = gpsimd_blocks(n)
+            hi = HB - AB
+            seeds(nxt[0])
             derive_group(cur)
-            if on_gpsimd(n):
-                root(cur[2])
-            if len(nxt) >= 2:
-                seeds(nxt[1])
-            if len(nxt) >= 3:
-                seeds(nxt[2])
+            root(cur[2], HB)
+            root(cur[1], pb)
+            second_scalar(cur[0], 0, HB)
+            second_scalar(cur[1], hi, HB)
+            for i in nxt[1:]:
+                seeds(i)
             for i in prev:
                 if i % SL == SL - 1:
-                    calls = calls + [(i // SL, first) for first in range(0, HP, QP)]
-            big = []
-            if len(cur) >= 1:
-                big.append(lambda: second(nc.vector, cur[0], 0, HB))
-            if len(cur) >= 3 and not on_gpsimd(n):
-                big.append(lambda: second(nc.vector, cur[2], 0, HB))
+                    calls = calls + calls_of(i // SL)
             little = []
             for (h, s) in plan.get(n, []):
                 if s == 0:
@@ -278,14 +291,16 @@ def tile_rgchromahistblock_kernel(tc, x, out):
                 little.extend(stages[h][s])
             done = pending
             pending = []
-            take = calls[0:QMAX]
-            calls = calls[QMAX:]
+            credit = credit + QCALLS * GROUP
+            share = min(len(calls), credit // SL)
+            credit = credit - share * SL if calls else 0
+            take = calls[0:share]
+            calls = calls[share:]
             used = 0
-            for f in big:
-                f()
-                if used < len(little):
-                    little[used]()
-                    used += 1
+            if used < len(little):
+                little[used]()
+                used += 1
+            second(nc.vector, cur[1], pb, hi - LAST)
             for kb in done:
                 finish(kb)
             for (h, first) in take:
@@ -295,13 +310,29 @@ def tile_rgchromahistblock_kernel(tc, x, out):
                     used += 1
             for f in little[used:]:
                 f()
-            if on_gpsimd(n):
-                root_squared(cur[2])
-            if len(cur) >= 2:
-                second(nc.vector, cur[1], RB, HB)
-        for (h, first) in calls:
-            for kb in pending:
-                finish(kb)
+            root_squared(cur[2], HB, True)
+            root_squared(cur[1], pb, False)
+            second(nc.vector, cur[1], hi - LAST, hi)
+            third(cur[1], pb, hi, False)
+            third(cur[0], 0, HB, True)
+            third(cur[1], hi, HB, True)
+
+        cur = groups[NFULL]
+        derive_group(cur)
+        final = calls_of(HALVES - 1)
+        early = [c for c in final if 2 * (c[1] + QP) <= CUT]
+        for (r0, r1, ready) in ((0, CUT, calls), (CUT, HB, early)):
+            second_scalar(cur[0], r0, r1)
+            for i in cur[1:]:
+                second(nc.vector, i, r0, r1)
+            for (h, first) in ready:
+                for kb in pending:
+                    finish(kb)
+                pending = quantise(h, first)
+            for i in cur[1:]:
+                third(i, r0, r1, False)
+            third(cur[0], r0, r1, True)
+        for (h, first) in final[len(early):]:
             pending = quantise(h, first)
         for kb in pending:
             finish(kb)

@@ -28,13 +28,11 @@ S2 = (63.0 * SIGMA) ** 2
 NB = 8
 SL = BINS // NB
 TOTAL = HALVES * SL
-GROUP = 3
+GROUP = 4
 NFULL = TOTAL // GROUP - 1
 CUT = 48
-AB = 11
-PB_LONG = 24
-PB_SHORT = 12
-LAST = 20
+DB = 38
+PC = 74
 QP = 4
 QCALLS = (HP + QP - 1) // QP
 
@@ -47,9 +45,9 @@ def tile_rgchromahistblock_kernel(tc, x, out):
     outv = out.rearrange("b o i j -> i (b o) j")
     with ExitStack() as ctx:
         const = ctx.enter_context(tc.tile_pool(name="const", bufs=1))
-        xin = ctx.enter_context(tc.tile_pool(name="xin", bufs=3))
+        xin = ctx.enter_context(tc.tile_pool(name="xin", bufs=2))
         prep = ctx.enter_context(tc.tile_pool(name="prep", bufs=2))
-        napool = ctx.enter_context(tc.tile_pool(name="napool", bufs=4))
+        napool = ctx.enter_context(tc.tile_pool(name="napool", bufs=3))
         wpool = ctx.enter_context(tc.tile_pool(name="wpool", bufs=2))
         kpool = ctx.enter_context(tc.tile_pool(name="kpool", bufs=2))
         cpool = ctx.enter_context(tc.tile_pool(name="cpool", bufs=4))
@@ -140,9 +138,9 @@ def tile_rgchromahistblock_kernel(tc, x, out):
             return wt[i]
 
         def squared(i):
-            if i in (1, 2):
+            if i in (2, 3):
                 return NB
-            if (i % GROUP == 0 and i <= GROUP * NFULL) or i % SL == 0:
+            if i % GROUP == 0:
                 return 2
             return 0
 
@@ -168,9 +166,6 @@ def tile_rgchromahistblock_kernel(tc, x, out):
             for i in g:
                 for k in range(squared(i), NB):
                     derive(i, k)
-
-        def derivations(g):
-            return sum(NB - squared(i) for i in g)
 
         def rows(i, r0, r1):
             return wt[i][:, r0:r1, :].rearrange("p b e -> p (b e)")
@@ -241,10 +236,7 @@ def tile_rgchromahistblock_kernel(tc, x, out):
                 return [b // 4]
             return []
 
-        groups = [list(range(GROUP * n, GROUP * n + GROUP)) for n in range(NFULL)] + [list(range(GROUP * NFULL, TOTAL))]
-
-        def gpsimd_blocks(n):
-            return PB_LONG if derivations(groups[n + 1]) >= GROUP * NB - 2 else PB_SHORT
+        groups = [list(range(GROUP * n, GROUP * n + GROUP)) for n in range(NFULL + 1)]
 
         def calls_of(h):
             return [(h, first) for first in range(0, HP, QP)]
@@ -252,7 +244,7 @@ def tile_rgchromahistblock_kernel(tc, x, out):
         plan = {0: [(1, 1), (1, 2)]}
         for h in range(2, HALVES):
             for s in range(3):
-                c = (SL * (h - 2)) // GROUP + 1 + s
+                c = 2 * h - 4 + s
                 plan[c] = plan.get(c, []) + [(h, s)]
 
         load(0)
@@ -268,22 +260,15 @@ def tile_rgchromahistblock_kernel(tc, x, out):
         pending = []
         credit = 0
         for n in range(NFULL):
-            cur = groups[n]
-            prev = groups[n - 1] if n >= 1 else []
-            nxt = groups[n + 1]
-            pb = gpsimd_blocks(n)
-            hi = HB - AB
-            seeds(nxt[0])
-            derive_group(cur)
-            root(cur[2], HB)
-            root(cur[1], pb)
-            second_scalar(cur[0], 0, HB)
-            second_scalar(cur[1], hi, HB)
-            for i in nxt[1:]:
-                seeds(i)
-            for i in prev:
-                if i % SL == SL - 1:
-                    calls = calls + calls_of(i // SL)
+            sa, sb, sc, sd = groups[n]
+            seeds(groups[n + 1][0])
+            derive_group(groups[n])
+            root(sd, HB)
+            root(sc, PC)
+            second_scalar(sa, 0, HB)
+            second_scalar(sb, DB, HB)
+            if n >= 1 and groups[n - 1][GROUP - 1] % SL == SL - 1:
+                calls = calls + calls_of(groups[n - 1][0] // SL)
             little = []
             for (h, s) in plan.get(n, []):
                 if s == 0:
@@ -300,7 +285,7 @@ def tile_rgchromahistblock_kernel(tc, x, out):
             if used < len(little):
                 little[used]()
                 used += 1
-            second(nc.vector, cur[1], pb, hi - LAST)
+            second(nc.vector, sb, 0, DB)
             for kb in done:
                 finish(kb)
             for (h, first) in take:
@@ -310,12 +295,13 @@ def tile_rgchromahistblock_kernel(tc, x, out):
                     used += 1
             for f in little[used:]:
                 f()
-            root_squared(cur[2], HB, True)
-            root_squared(cur[1], pb, False)
-            second(nc.vector, cur[1], hi - LAST, hi)
-            third(cur[1], pb, hi, False)
-            third(cur[0], 0, HB, True)
-            third(cur[1], hi, HB, True)
+            root_squared(sd, HB, True)
+            root_squared(sc, PC, False)
+            second(nc.vector, sc, PC, HB)
+            third(sb, 0, DB, False)
+            third(sa, 0, HB, True)
+            third(sb, DB, HB, True)
+            third(sc, PC, HB, False)
 
         cur = groups[NFULL]
         derive_group(cur)

@@ -5,7 +5,6 @@ from concourse.masks import make_identity
 
 F32 = mybir.dt.float32
 BF16 = mybir.dt.bfloat16
-I32 = mybir.dt.int32
 U32 = mybir.dt.uint32
 U8 = mybir.dt.uint8
 FP8X4 = mybir.dt.float8_e4m3fn_x4
@@ -19,306 +18,365 @@ PIXELS = 224 * 224
 BINS = 64
 EPS = 1e-6
 SIGMA = 0.02
-SLOTS = PIXELS // P
-HALVES = 2 * IMAGES
-HS = SLOTS // 2
-HP = HS // 4
-HB = 2 * HP
+ROWS = PIXELS // P
+TILES = IMAGES * ROWS // P
+PASSES_TILE = P // 4
+PASSES_IMAGE = ROWS // 4
+BT = 2 * PASSES_TILE
 S2 = (63.0 * SIGMA) ** 2
-NB = 8
-SL = BINS // NB
-TOTAL = HALVES * SL
-GROUP = 4
-NFULL = TOTAL // GROUP - 1
-CUT = 48
-DB = 38
-PC = 74
-QP = 4
-QCALLS = (HP + QP - 1) // QP
+TSQ = S2 + 1.0
+KAPPA = 4.0 * S2 + 4.0
+CHUNKS = 4
+QP = 8
+SEEDS = (-4, 28)
+GA = 64
+SA = 104
 
 FLOPS = 2 * IMAGES * PIXELS * BINS * BINS
 
 
 def tile_rgchromahistblock_kernel(tc, x, out):
     nc = tc.nc
-    xv = x.rearrange("b c h w -> b c (h w)").rearrange("b c (p t) -> p b c t", p=P)
-    outv = out.rearrange("b o i j -> i (b o) j")
+    xv = x.rearrange("b c h w -> b c (h w)").rearrange("b c (r w) -> b r c w", w=P)
+    outv = out.rearrange("b o (y g) j -> g y (b o) j", g=4)
     with ExitStack() as ctx:
         const = ctx.enter_context(tc.tile_pool(name="const", bufs=1))
         xin = ctx.enter_context(tc.tile_pool(name="xin", bufs=2))
-        prep = ctx.enter_context(tc.tile_pool(name="prep", bufs=2))
-        napool = ctx.enter_context(tc.tile_pool(name="napool", bufs=3))
+        prep = ctx.enter_context(tc.tile_pool(name="prep", bufs=1))
+        lpool = ctx.enter_context(tc.tile_pool(name="lpool", bufs=2))
+        sqpool = ctx.enter_context(tc.tile_pool(name="sqpool", bufs=2))
         wpool = ctx.enter_context(tc.tile_pool(name="wpool", bufs=2))
+        xpool = ctx.enter_context(tc.tile_pool(name="xpool", bufs=2))
+        rpool = ctx.enter_context(tc.tile_pool(name="rpool", bufs=2))
         kpool = ctx.enter_context(tc.tile_pool(name="kpool", bufs=2))
-        cpool = ctx.enter_context(tc.tile_pool(name="cpool", bufs=4))
-        small = ctx.enter_context(tc.tile_pool(name="small", bufs=2))
-        accp = ctx.enter_context(tc.psum_pool(name="accp", bufs=1))
-        d4pool = ctx.enter_context(tc.psum_pool(name="d4pool", bufs=2))
-        totp = ctx.enter_context(tc.psum_pool(name="totp", bufs=2))
+        cpool = ctx.enter_context(tc.tile_pool(name="cpool", bufs=2))
+        small = ctx.enter_context(tc.tile_pool(name="small", bufs=1))
+        accp = ctx.enter_context(tc.psum_pool(name="accp", bufs=2))
+        xps = ctx.enter_context(tc.psum_pool(name="xps", bufs=2))
+        ring = ctx.enter_context(tc.psum_pool(name="ring", bufs=4))
         ctx.enter_context(tc.manual_schedule())
 
-        ji = const.tile([P, BINS], I32)
-        nc.gpsimd.iota(out=ji[:], pattern=[[1, BINS]], base=0, channel_multiplier=0)
         ident = const.tile([P, P], F32)
         make_identity(nc, ident[:])
-        negj = const.tile([P, BINS], F32)
-        nc.vector.tensor_scalar(out=negj[:], in0=ji[:], scalar1=-1.0, scalar2=None, op0=ALU.mult)
-        one = const.tile([P, 1], F32)
-        nc.vector.memset(one[:], 1.0)
+        identv = ident[:].rearrange("p (s t) -> p s t", t=4)
         sel = const.tile([P, P], F32)
         nc.vector.memset(sel[0:64, :], 1.0)
         nc.vector.memset(sel[64:128, :], 0.0)
-        acc = [accp.tile([P, 512], F32, name="acc%d" % i) for i in range(4)]
+        zero = const.tile([P, 1], F32)
+        nc.vector.memset(zero[:], 0.0)
+        cbias = const.tile([P, 32], F32)
+        columns = {}
+
+        def bias(value):
+            if value not in columns:
+                n = len(columns)
+                nc.vector.tensor_scalar(out=cbias[:, n:n + 1], in0=zero[:], scalar1=value, scalar2=None, op0=ALU.add)
+                columns[value] = n
+            n = columns[value]
+            return cbias[:, n:n + 1]
+
+        units = [[2 * u + v for v in range(2) if 2 * u + v < TILES] for u in range((TILES + 1) // 2)]
+        steps = [(u, q) for u in range(len(units)) for q in range(CHUNKS)]
 
         xt = {}
-        na = {}
-        d4 = {}
-        wt = {}
+        n8 = {}
+        n16 = {}
+        sq = {}
+        xb = {}
+        seeds = {}
+        ws = {}
+        xx = {}
+        rr = {}
         kt = {}
+        acc = {}
         stages = {}
 
-        def load(b):
-            xb = xin.tile([P, 3, SLOTS], BF16)
-            nc.sync.dma_start(out=xb[:], in_=xv[:, b])
-            xt[b] = xb
+        def nrows(u):
+            return BT * len(units[u])
 
-        def prepare(h):
-            b, hi = divmod(h, 2)
-            if hi == 0 and b + 1 < IMAGES:
-                load(b + 1)
-            cl = prep.tile([P, 3, HS], BF16)
-            s1 = prep.tile([P, HS], F32)
-            s2 = prep.tile([P, HS], F32)
-            m = prep.tile([P, HS], F32)
-            y0 = prep.tile([P, HS], F32)
-            e = prep.tile([P, HS], F32)
-            yn = prep.tile([P, HS], F32)
-            xs = xt[b][:, :, hi * HS:(hi + 1) * HS]
-            ynv = yn[:].rearrange("p (c j) -> p c j", j=4)
+        def load(u):
+            xu = xin.tile([P, 2, 3, P], BF16)
+            xt[u] = xu
+            for v, tile in enumerate(units[u]):
+                done = 0
+                while done < P:
+                    b, r = divmod(tile * P + done, ROWS)
+                    n = min(P - done, ROWS - r)
+                    nc.sync.dma_start(out=xu[done:done + n, v], in_=xv[b, r:r + n])
+                    done += n
+
+        def prepare(u):
+            nt = len(units[u])
+            cl = prep.tile([P, 2, 3, P], BF16)
+            s1 = prep.tile([P, 2, P], F32)
+            s2 = prep.tile([P, 2, P], F32)
+            m = prep.tile([P, 2, P], F32)
+            y0 = prep.tile([P, 2, P], F32)
+            t8 = lpool.tile([P, 2, 2, P], F32)
+            t16 = lpool.tile([P, 2, 2, P], F32)
+            n8[u] = t8
+            n16[u] = t16
+            xs = xt[u]
 
             def chroma(ch):
-                if ch == 0:
-                    nah = napool.tile([P, HP, 2, 4], F32)
-                    na[h] = nah
-                nc.vector.scalar_tensor_tensor(
-                    out=na[h][:, :, ch, :], in0=cl[:, ch, :].rearrange("p (c j) -> p c j", j=4), scalar=252.0, in1=ynv,
-                    op0=ALU.mult, op1=ALU.mult)
+                nc.vector.scalar_tensor_tensor(out=t8[:, 0:nt, ch, :], in0=cl[:, 0:nt, ch, :], scalar=504.0, in1=m[:, 0:nt],
+                                               op0=ALU.mult, op1=ALU.mult)
 
-            def to_psum():
-                dp = d4pool.tile([P, 512], F32)
-                d4[h] = dp
-                nc.tensor.matmul(out=dp[:, 0:2 * HS], lhsT=ident[:], rhs=na[h][:].rearrange("p c h j -> p (c h j)"),
-                                 start=True, stop=True)
-
-            stages[h] = [
+            stages[u] = [
                 [
-                    lambda: nc.vector.tensor_scalar(out=cl[:], in0=xs, scalar1=0.0, scalar2=1.0, op0=ALU.max, op1=ALU.min),
-                    lambda: nc.vector.scalar_tensor_tensor(out=s1[:], in0=cl[:, 0, :], scalar=EPS, in1=cl[:, 1, :],
-                                                           op0=ALU.add, op1=ALU.add),
-                    lambda: nc.vector.tensor_tensor(out=s2[:], in0=s1[:], in1=cl[:, 2, :], op=ALU.add),
-                    lambda: nc.scalar.activation(out=m[:], in_=s2[:], func=ACTF.Abs_reciprocal_sqrt, scale=1.0),
+                    lambda: nc.vector.tensor_scalar(out=cl[:, 0:nt], in0=xs[:, 0:nt], scalar1=0.0, scalar2=1.0,
+                                                    op0=ALU.max, op1=ALU.min),
+                    lambda: nc.vector.scalar_tensor_tensor(out=s1[:, 0:nt], in0=cl[:, 0:nt, 0, :], scalar=EPS,
+                                                           in1=cl[:, 0:nt, 1, :], op0=ALU.add, op1=ALU.add),
+                    lambda: nc.vector.tensor_tensor(out=s2[:, 0:nt], in0=s1[:, 0:nt], in1=cl[:, 0:nt, 2, :], op=ALU.add),
                 ],
                 [
-                    lambda: nc.vector.tensor_tensor(out=y0[:], in0=m[:], in1=m[:], op=ALU.mult),
-                    lambda: nc.vector.tensor_tensor(out=e[:], in0=s2[:], in1=y0[:], op=ALU.mult),
-                    lambda: nc.vector.scalar_tensor_tensor(out=yn[:], in0=e[:], scalar=2.0, in1=y0[:],
+                    lambda: nc.vector.tensor_tensor(out=y0[:, 0:nt], in0=m[:, 0:nt], in1=m[:, 0:nt], op=ALU.mult),
+                    lambda: nc.vector.tensor_tensor(out=s1[:, 0:nt], in0=s2[:, 0:nt], in1=y0[:, 0:nt], op=ALU.mult),
+                    lambda: nc.vector.scalar_tensor_tensor(out=m[:, 0:nt], in0=s1[:, 0:nt], scalar=2.0, in1=y0[:, 0:nt],
                                                            op0=ALU.subtract, op1=ALU.mult),
-                    lambda: chroma(0),
                 ],
                 [
+                    lambda: chroma(0),
                     lambda: chroma(1),
-                    to_psum,
+                    lambda: nc.vector.tensor_scalar(out=t16[:, 0:nt], in0=t8[:, 0:nt], scalar1=2.0, scalar2=None, op0=ALU.mult),
                 ],
+                [],
             ]
+            return lambda: nc.scalar.activation(out=m[:, 0:nt], in_=s2[:, 0:nt], func=ACTF.Abs_reciprocal_sqrt, scale=1.0)
 
-        def squares_tile(i):
-            if i not in wt:
-                w = wpool.tile([P, HB, 4 * NB], F32, tag="w%d" % (i % GROUP))
-                wt[i] = w
-            return wt[i]
+        def square(u, q):
+            nt = len(units[u])
+            t = sqpool.tile([P, 2, 2, P], F32)
+            sq[u, q] = t
+            nc.scalar.activation(out=t[:, 0:nt], in_=n8[u][:, 0:nt], func=ACTF.Square, bias=bias(-float(16 * q + 2)), scale=-0.125)
 
-        def squared(i):
-            if i in (2, 3):
-                return NB
-            if i % GROUP == 0:
-                return 2
-            return 0
+        def transposes(u, bank, sources):
+            view = bank[:].rearrange("p (v s c t) -> p v c s t", v=2, c=2, t=4)
+            for v in range(len(units[u])):
+                for ch in range(2):
+                    for n, src in enumerate(sources):
+                        nc.tensor.matmul(out=view[:, v, ch], lhsT=src[:, v, ch, :], rhs=identv, start=n == 0,
+                                         stop=n == len(sources) - 1, is_transpose=True)
 
-        def seeds(i):
-            if squared(i) == 0:
-                return
-            h, si = divmod(i, SL)
-            w = squares_tile(i)
-            dv = na[h][:].rearrange("p c h j -> p (c h) j")
-            for k in range(squared(i)):
-                nc.scalar.activation(out=w[:, :, 4 * k:4 * k + 4], in_=dv, func=ACTF.Square,
-                                     bias=negj[:, NB * si + k:NB * si + k + 1], scale=-0.25)
+        def chroma_bank(u):
+            bank = xps.tile([P, 512], F32)
+            xb[u] = bank
+            transposes(u, bank, [n8[u]])
 
-        def derive(i, k):
-            h, si = divmod(i, SL)
-            w = squares_tile(i)
-            before = w[:, :, 4 * k - 8:4 * k - 4] if k >= 2 else wt[i - 1][:, :, 4 * (NB + k) - 8:4 * (NB + k) - 4]
-            dv = d4[h][:, 0:2 * HS].rearrange("p (b j) -> p b j", j=4)
-            nc.vector.scalar_tensor_tensor(out=w[:, :, 4 * k:4 * k + 4], in0=dv, scalar=float(4 * (NB * si + k) - 4),
-                                           in1=before, op0=ALU.add, op1=ALU.add)
+        def block(bank, nb):
+            return bank[:, 0:4 * nb].rearrange("p (b t) -> p b t", t=4)
 
-        def derive_group(g):
-            for i in g:
-                for k in range(squared(i), NB):
-                    derive(i, k)
+        def make_seeds(u):
+            nb = nrows(u)
+            for i in SEEDS:
+                sd = small.tile([P, 512], F32, tag="seed%d" % (i + 4), name="seed")
+                seeds[u, i] = sd
+                nc.scalar.activation(out=sd[:, 0:4 * nb], in_=xb[u][:, 0:4 * nb], func=ACTF.Square, bias=bias(-float(i)), scale=-0.125)
 
-        def rows(i, r0, r1):
-            return wt[i][:, r0:r1, :].rearrange("p b e -> p (b e)")
+        def wslot(u, x4):
+            nb = nrows(u)
+            if x4 == 16:
+                if (u, 4) not in ws:
+                    w = wpool.tile([P, 512], F32, tag="wlast", bufs=1, name="wlast")
+                    ws[u, 4] = w
+                return block(ws[u, 4], nb)
+            q, k = divmod(x4, 4)
+            if (u, q) not in ws:
+                w = wpool.tile([P, 2 * BT, 16], F32, tag="ws", name="ws")
+                ws[u, q] = w
+            return ws[u, q][:, 0:nb, 4 * k:4 * k + 4]
 
-        def second(eng, i, r0, r1):
-            flat = rows(i, r0, r1)
-            eng.scalar_tensor_tensor(out=flat, in0=flat, scalar=2.0 * S2, in1=flat, op0=ALU.add, op1=ALU.mult)
-
-        def second_scalar(i, r0, r1):
-            flat = rows(i, r0, r1)
-            nc.scalar.activation(out=flat, in_=flat, func=ACTF.Square, bias=one[:], scale=1.0 / S2)
-
-        def kernel_values(i):
-            h, si = divmod(i, SL)
-            if h not in kt:
-                kh = kpool.tile([P, HB, 4 * BINS], BF16, align_bytes=64)
-                kt[h] = kh
-            return kt[h][:, :, 4 * NB * si:4 * NB * (si + 1)]
-
-        def root(i, r1):
-            flat = rows(i, 0, r1)
-            nc.scalar.activation(out=flat, in_=flat, func=ACTF.Abs_reciprocal_sqrt, bias=one[:], scale=1.0 / S2)
-
-        def root_squared(i, r1, hold):
-            dst = kernel_values(i)[:, 0:r1, :]
-            if hold:
-                nc.vector.memset(dst[:, 0, 0:16], 0.0)
-            nc.gpsimd.tensor_tensor(out=dst, in0=wt[i][:, 0:r1, :], in1=wt[i][:, 0:r1, :], op=ALU.mult)
-
-        def third(i, r0, r1, squared_by_scalar):
-            dst = kernel_values(i)[:, r0:r1, :]
-            if squared_by_scalar:
-                nc.scalar.activation(out=dst, in_=wt[i][:, r0:r1, :], func=ACTF.Abs_reciprocal_sqrt, scale=1.0)
+        def derive(u, x4):
+            nb = nrows(u)
+            i = 4 * x4
+            add = float(8 * i - 16)
+            if i - 4 in SEEDS:
+                before = block(seeds[u, i - 4], nb)
+                add = add + TSQ
             else:
-                nc.scalar.activation(out=dst, in_=wt[i][:, r0:r1, :], func=ACTF.Abs_reciprocal_sqrt,
-                                     bias=one[:], scale=1.0 / (S2 * S2))
+                before = wslot(u, x4 - 1)
+            nc.vector.scalar_tensor_tensor(out=wslot(u, x4), in0=block(xb[u], nb), scalar=add, in1=before,
+                                           op0=ALU.add, op1=ALU.add)
+
+        def bank_constant(k, q):
+            return float(2 * 4 * k * (16 * q + 2) + 16 * k * k)
+
+        def kview(u, r0, r1, q):
+            return kt[u][:].rearrange("p b (g q e) -> p b g q e", g=4, q=4)[:, r0:r1, :, q, :]
+
+        banks = {}
+
+        def fill(u, q):
+            for k in range(4):
+                bank = ring.tile([P, 512], F32)
+                banks[u, q, k] = bank
+                transposes(u, bank, [[sq[u, q]], [sq[u, q], n8[u]], [sq[u, q], n16[u]], [sq[u, q], n16[u], n8[u]]][k])
+
+        def products(u, q):
+            nb = nrows(u)
+            xq = xpool.tile([P, 2 * BT, 2, 16], F32)
+            xx[u, q] = xq
+            if q == 0:
+                derive(u, 0)
+            for k in range(4):
+                derive(u, 4 * q + k + 1)
+                for side in range(2):
+                    nc.vector.scalar_tensor_tensor(
+                        out=xq[:, 0:nb, side, 4 * k:4 * k + 4], in0=block(banks[u, q, k], nb), scalar=TSQ + bank_constant(k, q),
+                        in1=wslot(u, 4 * q + k + side), op0=ALU.add, op1=ALU.mult)
+
+        def roots(u, q):
+            nb = nrows(u)
+            r2 = rpool.tile([P, 2 * BT, 16], F32, tag="r2", name="r2")
+            r0 = rpool.tile([P, 2 * BT, 16], F32, tag="r0", bufs=1, name="r0")
+            rr[u, q] = (r0, r2)
+            for k in range(4):
+                nc.scalar.activation(out=r2[:, 0:nb, 4 * k:4 * k + 4], in_=block(banks[u, q, k], nb), func=ACTF.Abs_reciprocal_sqrt,
+                                     bias=bias(1.0 + bank_constant(k, q) / S2), scale=1.0 / S2)
+            nc.scalar.activation(out=r0[:, 0:nb], in_=ws[u, q][:, 0:nb, :], func=ACTF.Abs_reciprocal_sqrt,
+                                 bias=bias(-1.0 / S2), scale=1.0 / S2)
+
+        def from_products(u, q):
+            nb = nrows(u)
+            nc.scalar.activation(out=kview(u, 0, nb, q)[:, :, 1::2], in_=xx[u, q][:, 0:nb], func=ACTF.Abs_reciprocal_sqrt,
+                                 bias=bias(-KAPPA / (S2 * S2)), scale=1.0 / (S2 * S2))
+
+        def cuts(u):
+            return [c * len(units[u]) // 2 for c in (0, GA, SA, 2 * BT)]
+
+        def hold(u, q):
+            nc.vector.memset(kview(u, 0, 1, q)[:, 0, 2, :], 0.0)
+
+        def square_roots(eng, u, q, part):
+            c = cuts(u)
+            nb = nrows(u)
+            if part == 0:
+                src = rr[u, q][1][:, 0:nb]
+                nc.gpsimd.tensor_tensor(out=kview(u, 0, nb, q)[:, :, 2], in0=src, in1=src, op=ALU.mult)
+            src = rr[u, q][0][:, c[part]:c[part + 1]]
+            dst = kview(u, c[part], c[part + 1], q)[:, :, 0]
+            if part == 1:
+                nc.scalar.activation(out=dst, in_=src, func=ACTF.Square)
+            else:
+                eng.tensor_tensor(out=dst, in0=src, in1=src, op=ALU.mult)
 
         def finish(kb):
             hist = acc[kb][:].rearrange("p (i c) -> p i c", c=P)[:, :, BINS:P]
             rsum = small.tile([P, 4], F32)
             nc.vector.tensor_reduce(out=rsum[:], in_=hist, axis=AX.X, op=ALU.add)
-            tot = totp.tile([P, 4], F32)
-            nc.tensor.matmul(out=tot[:], lhsT=sel[:], rhs=rsum[:], start=True, stop=True)
+            tot = ring.tile([P, 512], F32, tag="bank", name="bank")
+            nc.tensor.matmul(out=tot[:, 0:4], lhsT=sel[:], rhs=rsum[:], start=True, stop=True)
             te = small.tile([P, 4], F32)
-            nc.vector.tensor_scalar(out=te[:], in0=tot[:], scalar1=EPS, scalar2=None, op0=ALU.add)
+            nc.vector.tensor_scalar(out=te[:], in0=tot[:, 0:4], scalar1=EPS, scalar2=None, op0=ALU.add)
             rt = small.tile([P, 4], F32)
             nc.vector.reciprocal(out=rt[:], in_=te[:])
             o = small.tile([BINS, 4, BINS], F32)
-            nc.vector.tensor_tensor(out=o[:], in0=hist[0:BINS], in1=rt[0:BINS, :].unsqueeze(2).to_broadcast([BINS, 4, BINS]),
-                                    op=ALU.mult)
-            nc.sync.dma_start(out=outv[:, 4 * kb:4 * kb + 4, :], in_=o[:])
+            for i in range(4):
+                nc.vector.tensor_scalar(out=o[:, i, :].rearrange("p (y g) -> p g y", g=4),
+                                        in0=hist[0:BINS, i, :].rearrange("p (g y) -> p g y", g=4),
+                                        scalar1=rt[0:BINS, i:i + 1], scalar2=None, op0=ALU.mult)
+            for g in range(4):
+                nc.sync.dma_start(out=outv[g, :, 4 * kb:4 * kb + 4, :], in_=o[16 * g:16 * g + 16])
 
-        def quantise(h, first):
-            n = min(QP, HP - first)
+        def quantise(u, first):
             codes = cpool.tile([P, QP * P], U32, align_bytes=64)
             scales = cpool.tile([P, QP * P], U8, align_bytes=64)
-            nc.vector.quantize_mx(out=codes[:, 0:n * P].bitcast(FP8X4), scales=scales[:, 0:n * P],
-                                  in_=kt[h][:, 2 * first:2 * (first + n), :].rearrange("p b e -> p (b e)"))
-            b, hi = divmod(h, 2)
-            for c in range(n):
+            nc.vector.quantize_mx(out=codes[:].bitcast(FP8X4), scales=scales[:],
+                                  in_=kt[u][:, 2 * first:2 * (first + QP), :].rearrange("p b e -> p (b e)"))
+            return (u, first, codes, scales)
+
+        def multiply(job):
+            u, first, codes, scales = job
+            complete = []
+            for c in range(QP):
+                b, n = divmod(units[u][0] * PASSES_TILE + first + c, PASSES_IMAGE)
+                if b % 4 == 0 and n == 0:
+                    a = accp.tile([P, 512], F32)
+                    acc[b // 4] = a
                 cols = slice(c * P, (c + 1) * P)
                 nc.tensor.matmul_mx(
                     out=acc[b // 4][:, (b % 4) * P:(b % 4 + 1) * P],
                     lhsT=codes[:, cols].bitcast(FP8X4), lhsT_scale=scales[:, cols],
                     rhs=codes[:, cols].bitcast(FP8X4), rhs_scale=scales[:, cols],
-                    start=(hi == 0 and first + c == 0), stop=(hi == 1 and first + c == HP - 1))
-            if hi == 1 and first + n == HP and b % 4 == 3:
-                return [b // 4]
-            return []
-
-        groups = [list(range(GROUP * n, GROUP * n + GROUP)) for n in range(NFULL + 1)]
-
-        def calls_of(h):
-            return [(h, first) for first in range(0, HP, QP)]
-
-        plan = {0: [(1, 1), (1, 2)]}
-        for h in range(2, HALVES):
-            for s in range(3):
-                c = 2 * h - 4 + s
-                plan[c] = plan.get(c, []) + [(h, s)]
+                    start=n == 0, stop=n == PASSES_IMAGE - 1)
+                if b % 4 == 3 and n == PASSES_IMAGE - 1:
+                    complete.append(b // 4)
+            return complete
 
         load(0)
-        prepare(0)
-        prepare(1)
-        for st in (stages[0][0], stages[1][0], stages[0][1], stages[0][2]):
-            for f in st:
-                f()
-        for i in groups[0]:
-            seeds(i)
+        load(1)
+        root = prepare(0)
+        for f in stages[0][0]:
+            f()
+        root()
+        for f in stages[0][1] + stages[0][2]:
+            f()
+        square(0, 0)
+        chroma_bank(0)
+        make_seeds(0)
 
         calls = []
-        pending = []
-        credit = 0
-        for n in range(NFULL):
-            sa, sb, sc, sd = groups[n]
-            seeds(groups[n + 1][0])
-            derive_group(groups[n])
-            root(sd, HB)
-            root(sc, PC)
-            second_scalar(sa, 0, HB)
-            second_scalar(sb, DB, HB)
-            if n >= 1 and groups[n - 1][GROUP - 1] % SL == SL - 1:
-                calls = calls + calls_of(groups[n - 1][0] // SL)
-            little = []
-            for (h, s) in plan.get(n, []):
-                if s == 0:
-                    prepare(h)
-                little.extend(stages[h][s])
-            done = pending
-            pending = []
-            credit = credit + QCALLS * GROUP
-            share = min(len(calls), credit // SL)
-            credit = credit - share * SL if calls else 0
-            take = calls[0:share]
+        jobs = []
+        done = []
+        root = None
+        prior = None
+        for u, q in steps:
+            last = u == len(units) - 1
+            if q == 0 and not last:
+                root = prepare(u + 1)
+            fill(u, q)
+            for job in jobs:
+                done = done + multiply(job)
+            jobs = []
+            if q == 3 and not last:
+                chroma_bank(u + 1)
+            if prior is not None:
+                square_roots(nc.gpsimd, prior[0], prior[1], 0)
+            if prior is not None:
+                from_products(prior[0], prior[1])
+                square_roots(nc.scalar, prior[0], prior[1], 1)
+            if q == 1 and not last:
+                root()
+            if q < 3:
+                square(u, q + 1)
+            elif not last:
+                square(u + 1, 0)
+                make_seeds(u + 1)
+            products(u, q)
+            roots(u, q)
+            if prior is not None:
+                square_roots(nc.vector, prior[0], prior[1], 2)
+            finished = done
+            done = []
+            if not last:
+                for f in stages[u + 1][q]:
+                    f()
+            if q == 1 and u >= 1:
+                calls = calls + [(u - 1, first) for first in range(0, PASSES_TILE * len(units[u - 1]), QP)]
+            share = min(len(calls), 2)
+            for call in calls[0:share]:
+                jobs.append(quantise(call[0], call[1]))
             calls = calls[share:]
-            used = 0
-            if used < len(little):
-                little[used]()
-                used += 1
-            second(nc.vector, sb, 0, DB)
-            for kb in done:
+            for kb in finished:
                 finish(kb)
-            for (h, first) in take:
-                pending = pending + quantise(h, first)
-                if used < len(little):
-                    little[used]()
-                    used += 1
-            for f in little[used:]:
-                f()
-            root_squared(sd, HB, True)
-            root_squared(sc, PC, False)
-            second(nc.vector, sc, PC, HB)
-            third(sb, 0, DB, False)
-            third(sa, 0, HB, True)
-            third(sb, DB, HB, True)
-            third(sc, PC, HB, False)
+            if q == 0:
+                kh = kpool.tile([P, 2 * BT, 4 * BINS], BF16, align_bytes=64)
+                kt[u] = kh
+            hold(u, q)
+            if q == 1 and u + 2 < len(units):
+                load(u + 2)
+            prior = (u, q)
 
-        cur = groups[NFULL]
-        derive_group(cur)
-        final = calls_of(HALVES - 1)
-        early = [c for c in final if 2 * (c[1] + QP) <= CUT]
-        for (r0, r1, ready) in ((0, CUT, calls), (CUT, HB, early)):
-            second_scalar(cur[0], r0, r1)
-            for i in cur[1:]:
-                second(nc.vector, i, r0, r1)
-            for (h, first) in ready:
-                for kb in pending:
-                    finish(kb)
-                pending = quantise(h, first)
-            for i in cur[1:]:
-                third(i, r0, r1, False)
-            third(cur[0], r0, r1, True)
-        for (h, first) in final[len(early):]:
-            pending = quantise(h, first)
-        for kb in pending:
+        u, q = prior
+        for job in jobs:
+            done = done + multiply(job)
+        square_roots(nc.gpsimd, u, q, 0)
+        from_products(u, q)
+        square_roots(nc.scalar, u, q, 1)
+        square_roots(nc.vector, u, q, 2)
+        calls = calls + [(u, first) for first in range(0, PASSES_TILE * len(units[u]), QP)]
+        for call in calls:
+            done = done + multiply(quantise(call[0], call[1]))
+        for kb in done:
             finish(kb)

@@ -30,7 +30,6 @@ CHUNKS = 4
 QP = 8
 SEEDS = (-4, 28)
 GA = 64
-SA = 104
 
 FLOPS = 2 * IMAGES * PIXELS * BINS * BINS
 
@@ -145,11 +144,11 @@ def tile_rgchromahistblock_kernel(tc, x, out):
             ]
             return lambda: nc.scalar.activation(out=m[:, 0:nt], in_=s2[:, 0:nt], func=ACTF.Abs_reciprocal_sqrt, scale=1.0)
 
-        def square(u, q):
+        def square(u, h):
             nt = len(units[u])
             t = sqpool.tile([P, 2, 2, P], F32)
-            sq[u, q] = t
-            nc.scalar.activation(out=t[:, 0:nt], in_=n8[u][:, 0:nt], func=ACTF.Square, bias=bias(-float(16 * q + 2)), scale=-0.125)
+            sq[u, h] = t
+            nc.scalar.activation(out=t[:, 0:nt], in_=n8[u][:, 0:nt], func=ACTF.Square, bias=bias(-float(32 * h + 2)), scale=-0.125)
 
         def transposes(u, bank, sources):
             view = bank[:].rearrange("p (v s c t) -> p v c s t", v=2, c=2, t=4)
@@ -200,7 +199,9 @@ def tile_rgchromahistblock_kernel(tc, x, out):
                                            op0=ALU.add, op1=ALU.add)
 
         def bank_constant(k, q):
-            return float(2 * 4 * k * (16 * q + 2) + 16 * k * k)
+            h, odd = divmod(q, 2)
+            m = 16 * odd + 4 * k
+            return float(2 * m * (32 * h + 2) + m * m)
 
         def kview(u, r0, r1, q):
             return kt[u][:].rearrange("p b (g q e) -> p b g q e", g=4, q=4)[:, r0:r1, :, q, :]
@@ -211,7 +212,8 @@ def tile_rgchromahistblock_kernel(tc, x, out):
             for k in range(4):
                 bank = ring.tile([P, 512], F32)
                 banks[u, q, k] = bank
-                transposes(u, bank, [[sq[u, q]], [sq[u, q], n8[u]], [sq[u, q], n16[u]], [sq[u, q], n16[u], n8[u]]][k])
+                n = 4 * (q % 2) + k
+                transposes(u, bank, [sq[u, q // 2]] + [n16[u]] * (n // 2) + [n8[u]] * (n % 2))
 
         def products(u, q):
             nb = nrows(u)
@@ -243,12 +245,12 @@ def tile_rgchromahistblock_kernel(tc, x, out):
                                  bias=bias(-KAPPA / (S2 * S2)), scale=1.0 / (S2 * S2))
 
         def cuts(u):
-            return [c * len(units[u]) // 2 for c in (0, GA, SA, 2 * BT)]
+            return [c * len(units[u]) // 2 for c in (0, GA, 2 * BT)]
 
         def hold(u, q):
             nc.vector.memset(kview(u, 0, 1, q)[:, 0, 2, :], 0.0)
 
-        def square_roots(eng, u, q, part):
+        def square_roots(u, q, part):
             c = cuts(u)
             nb = nrows(u)
             if part == 0:
@@ -259,7 +261,7 @@ def tile_rgchromahistblock_kernel(tc, x, out):
             if part == 1:
                 nc.scalar.activation(out=dst, in_=src, func=ACTF.Square)
             else:
-                eng.tensor_tensor(out=dst, in0=src, in1=src, op=ALU.mult)
+                nc.gpsimd.tensor_tensor(out=dst, in0=src, in1=src, op=ALU.mult)
 
         def finish(kb):
             hist = acc[kb][:].rearrange("p (i c) -> p i c", c=P)[:, :, BINS:P]
@@ -332,31 +334,30 @@ def tile_rgchromahistblock_kernel(tc, x, out):
             if q == 3 and not last:
                 chroma_bank(u + 1)
             if prior is not None:
-                square_roots(nc.gpsimd, prior[0], prior[1], 0)
+                square_roots(prior[0], prior[1], 0)
             if prior is not None:
                 from_products(prior[0], prior[1])
-                square_roots(nc.scalar, prior[0], prior[1], 1)
+                square_roots(prior[0], prior[1], 1)
             if q == 1 and not last:
                 root()
-            if q < 3:
-                square(u, q + 1)
-            elif not last:
+            if q == 1:
+                square(u, 1)
+            elif q == 3 and not last:
                 square(u + 1, 0)
                 make_seeds(u + 1)
             products(u, q)
             roots(u, q)
-            if prior is not None:
-                square_roots(nc.vector, prior[0], prior[1], 2)
             finished = done
             done = []
-            if not last:
-                for f in stages[u + 1][q]:
-                    f()
+            little = [] if last else stages[u + 1][q]
             if q == 1 and u >= 1:
                 calls = calls + [(u - 1, first) for first in range(0, PASSES_TILE * len(units[u - 1]), QP)]
             share = min(len(calls), 2)
-            for call in calls[0:share]:
-                jobs.append(quantise(call[0], call[1]))
+            for n in range(max(share, len(little))):
+                if n < len(little):
+                    little[n]()
+                if n < share:
+                    jobs.append(quantise(calls[n][0], calls[n][1]))
             calls = calls[share:]
             for kb in finished:
                 finish(kb)
@@ -371,10 +372,9 @@ def tile_rgchromahistblock_kernel(tc, x, out):
         u, q = prior
         for job in jobs:
             done = done + multiply(job)
-        square_roots(nc.gpsimd, u, q, 0)
+        square_roots(u, q, 0)
         from_products(u, q)
-        square_roots(nc.scalar, u, q, 1)
-        square_roots(nc.vector, u, q, 2)
+        square_roots(u, q, 1)
         calls = calls + [(u, first) for first in range(0, PASSES_TILE * len(units[u]), QP)]
         for call in calls:
             done = done + multiply(quantise(call[0], call[1]))

@@ -28,8 +28,9 @@ TSQ = S2 + 1.0
 KAPPA = 4.0 * S2 + 4.0
 CHUNKS = 4
 QP = 8
-SEEDS = (-4, 28)
-GA = 64
+SEEDS = (-4,)
+GA = 56
+SA = 110
 
 FLOPS = 2 * IMAGES * PIXELS * BINS * BINS
 
@@ -66,6 +67,11 @@ def tile_rgchromahistblock_kernel(tc, x, out):
         cbias = const.tile([P, 32], F32)
         columns = {}
 
+        def bank_constant(k, q):
+            h, odd = divmod(q, 2)
+            m = 16 * odd + 4 * k
+            return float(2 * m * (32 * h + 2) + m * m)
+
         def bias(value):
             if value not in columns:
                 n = len(columns)
@@ -73,6 +79,10 @@ def tile_rgchromahistblock_kernel(tc, x, out):
                 columns[value] = n
             n = columns[value]
             return cbias[:, n:n + 1]
+
+        for value in ([-2.0, 4.0, -34.0, -KAPPA / (S2 * S2), -1.0 / S2]
+                      + [1.0 + bank_constant(k, q) / S2 for q in range(CHUNKS) for k in range(4)]):
+            bias(value)
 
         units = [[2 * u + v for v in range(2) if 2 * u + v < TILES] for u in range((TILES + 1) // 2)]
         steps = [(u, q) for u in range(len(units)) for q in range(CHUNKS)]
@@ -198,11 +208,6 @@ def tile_rgchromahistblock_kernel(tc, x, out):
             nc.vector.scalar_tensor_tensor(out=wslot(u, x4), in0=block(xb[u], nb), scalar=add, in1=before,
                                            op0=ALU.add, op1=ALU.add)
 
-        def bank_constant(k, q):
-            h, odd = divmod(q, 2)
-            m = 16 * odd + 4 * k
-            return float(2 * m * (32 * h + 2) + m * m)
-
         def kview(u, r0, r1, q):
             return kt[u][:].rearrange("p b (g q e) -> p b g q e", g=4, q=4)[:, r0:r1, :, q, :]
 
@@ -245,7 +250,7 @@ def tile_rgchromahistblock_kernel(tc, x, out):
                                  bias=bias(-KAPPA / (S2 * S2)), scale=1.0 / (S2 * S2))
 
         def cuts(u):
-            return [c * len(units[u]) // 2 for c in (0, GA, 2 * BT)]
+            return [c * len(units[u]) // 2 for c in (0, GA, SA, 2 * BT)]
 
         def hold(u, q):
             nc.vector.memset(kview(u, 0, 1, q)[:, 0, 2, :], 0.0)
@@ -261,7 +266,7 @@ def tile_rgchromahistblock_kernel(tc, x, out):
             if part == 1:
                 nc.scalar.activation(out=dst, in_=src, func=ACTF.Square)
             else:
-                nc.gpsimd.tensor_tensor(out=dst, in0=src, in1=src, op=ALU.mult)
+                (nc.vector if part == 2 else nc.gpsimd).tensor_tensor(out=dst, in0=src, in1=src, op=ALU.mult)
 
         def finish(kb):
             hist = acc[kb][:].rearrange("p (i c) -> p i c", c=P)[:, :, BINS:P]
@@ -346,7 +351,6 @@ def tile_rgchromahistblock_kernel(tc, x, out):
                 square(u + 1, 0)
                 make_seeds(u + 1)
             products(u, q)
-            roots(u, q)
             finished = done
             done = []
             little = [] if last else stages[u + 1][q]
@@ -358,13 +362,19 @@ def tile_rgchromahistblock_kernel(tc, x, out):
                     little[n]()
                 if n < share:
                     jobs.append(quantise(calls[n][0], calls[n][1]))
+                if n == 0 and prior is not None:
+                    square_roots(prior[0], prior[1], 2)
+            if max(share, len(little)) == 0 and prior is not None:
+                square_roots(prior[0], prior[1], 2)
             calls = calls[share:]
+            roots(u, q)
             for kb in finished:
                 finish(kb)
             if q == 0:
                 kh = kpool.tile([P, 2 * BT, 4 * BINS], BF16, align_bytes=64)
                 kt[u] = kh
-            hold(u, q)
+            if (u, q) != steps[-1]:
+                hold(u, q)
             if q == 1 and u + 2 < len(units):
                 load(u + 2)
             prior = (u, q)
@@ -372,9 +382,11 @@ def tile_rgchromahistblock_kernel(tc, x, out):
         u, q = prior
         for job in jobs:
             done = done + multiply(job)
-        square_roots(u, q, 0)
         from_products(u, q)
-        square_roots(u, q, 1)
+        nb = nrows(u)
+        for e2 in range(2):
+            src = rr[u, q][e2][:, 0:nb]
+            nc.vector.tensor_tensor(out=kview(u, 0, nb, q)[:, :, 2 * e2], in0=src, in1=src, op=ALU.mult)
         calls = calls + [(u, first) for first in range(0, PASSES_TILE * len(units[u]), QP)]
         for call in calls:
             done = done + multiply(quantise(call[0], call[1]))

@@ -233,20 +233,23 @@ def tile_rgchromahistblock_kernel(tc, x, out):
                         out=xq[:, 0:nb, side, 4 * k:4 * k + 4], in0=block(banks[u, q, k], nb), scalar=TSQ + bank_constant(k, q),
                         in1=wslot(u, 4 * q + k + side), op0=ALU.add, op1=ALU.mult)
 
-        def roots(u, q):
+        def bank_root(u, q, k):
             nb = nrows(u)
-            r2 = rpool.tile([P, 2 * BT, 16], F32, tag="r2", name="r2")
+            if k == 0:
+                r2 = rpool.tile([P, 2 * BT, 16], F32, tag="r2", name="r2")
+                rr[u, q] = [None, r2]
+            nc.scalar.activation(out=rr[u, q][1][:, 0:nb, 4 * k:4 * k + 4], in_=block(banks[u, q, k], nb),
+                                 func=ACTF.Abs_reciprocal_sqrt, bias=bias(1.0 + bank_constant(k, q) / S2), scale=1.0 / S2)
+
+        def chain_roots(u, q):
+            nb = nrows(u)
             r0 = rpool.tile([P, 2 * BT, 16], F32, tag="r0", bufs=1, name="r0")
-            rr[u, q] = (r0, r2)
-            for k in range(4):
-                nc.scalar.activation(out=r2[:, 0:nb, 4 * k:4 * k + 4], in_=block(banks[u, q, k], nb), func=ACTF.Abs_reciprocal_sqrt,
-                                     bias=bias(1.0 + bank_constant(k, q) / S2), scale=1.0 / S2)
+            rr[u, q][0] = r0
             nc.scalar.activation(out=r0[:, 0:nb], in_=ws[u, q][:, 0:nb, :], func=ACTF.Abs_reciprocal_sqrt,
                                  bias=bias(-1.0 / S2), scale=1.0 / S2)
 
-        def from_products(u, q):
-            nb = nrows(u)
-            nc.scalar.activation(out=kview(u, 0, nb, q)[:, :, 1::2], in_=xx[u, q][:, 0:nb], func=ACTF.Abs_reciprocal_sqrt,
+        def from_products(u, q, r0, r1):
+            nc.scalar.activation(out=kview(u, r0, r1, q)[:, :, 1::2], in_=xx[u, q][:, r0:r1], func=ACTF.Abs_reciprocal_sqrt,
                                  bias=bias(-KAPPA / (S2 * S2)), scale=1.0 / (S2 * S2))
 
         def cuts(u):
@@ -340,17 +343,26 @@ def tile_rgchromahistblock_kernel(tc, x, out):
                 chroma_bank(u + 1)
             if prior is not None:
                 square_roots(prior[0], prior[1], 0)
+            products(u, q)
+            half = 0
             if prior is not None:
-                from_products(prior[0], prior[1])
+                half = nrows(prior[0]) // 2
+                from_products(prior[0], prior[1], 0, half)
+            bank_root(u, q, 0)
+            if prior is not None:
                 square_roots(prior[0], prior[1], 1)
             if q == 1 and not last:
                 root()
+            bank_root(u, q, 1)
             if q == 1:
                 square(u, 1)
             elif q == 3 and not last:
                 square(u + 1, 0)
                 make_seeds(u + 1)
-            products(u, q)
+            if prior is not None:
+                from_products(prior[0], prior[1], half, 2 * half)
+            bank_root(u, q, 2)
+            bank_root(u, q, 3)
             finished = done
             done = []
             little = [] if last else stages[u + 1][q]
@@ -367,7 +379,7 @@ def tile_rgchromahistblock_kernel(tc, x, out):
             if max(share, len(little)) == 0 and prior is not None:
                 square_roots(prior[0], prior[1], 2)
             calls = calls[share:]
-            roots(u, q)
+            chain_roots(u, q)
             for kb in finished:
                 finish(kb)
             if q == 0:
@@ -382,7 +394,7 @@ def tile_rgchromahistblock_kernel(tc, x, out):
         u, q = prior
         for job in jobs:
             done = done + multiply(job)
-        from_products(u, q)
+        from_products(u, q, 0, nrows(u))
         nb = nrows(u)
         for e2 in range(2):
             src = rr[u, q][e2][:, 0:nb]

@@ -28,9 +28,9 @@ TSQ = S2 + 1.0
 KAPPA = 4.0 * S2 + 4.0
 CHUNKS = 4
 QP = 8
-SEEDS = (-4,)
+SEEDS = (-4, 28)
 GA = 56
-SA = 110
+SA = 106
 
 FLOPS = 2 * IMAGES * PIXELS * BINS * BINS
 
@@ -80,7 +80,7 @@ def tile_rgchromahistblock_kernel(tc, x, out):
             n = columns[value]
             return cbias[:, n:n + 1]
 
-        for value in ([-2.0, 4.0, -34.0, -KAPPA / (S2 * S2), -1.0 / S2]
+        for value in ([-2.0, 4.0, -28.0, -34.0, -KAPPA / (S2 * S2), -1.0 / S2]
                       + [1.0 + bank_constant(k, q) / S2 for q in range(CHUNKS) for k in range(4)]):
             bias(value)
 
@@ -89,7 +89,7 @@ def tile_rgchromahistblock_kernel(tc, x, out):
 
         xt = {}
         n8 = {}
-        n16 = {}
+        n24 = {}
         sq = {}
         xb = {}
         seeds = {}
@@ -122,9 +122,9 @@ def tile_rgchromahistblock_kernel(tc, x, out):
             m = prep.tile([P, 2, P], F32)
             y0 = prep.tile([P, 2, P], F32)
             t8 = lpool.tile([P, 2, 2, P], F32)
-            t16 = lpool.tile([P, 2, 2, P], F32)
+            t24 = lpool.tile([P, 2, 2, P], F32)
             n8[u] = t8
-            n16[u] = t16
+            n24[u] = t24
             xs = xt[u]
 
             def chroma(ch):
@@ -148,7 +148,7 @@ def tile_rgchromahistblock_kernel(tc, x, out):
                 [
                     lambda: chroma(0),
                     lambda: chroma(1),
-                    lambda: nc.vector.tensor_scalar(out=t16[:, 0:nt], in0=t8[:, 0:nt], scalar1=2.0, scalar2=None, op0=ALU.mult),
+                    lambda: nc.vector.tensor_scalar(out=t24[:, 0:nt], in0=t8[:, 0:nt], scalar1=3.0, scalar2=None, op0=ALU.mult),
                 ],
                 [],
             ]
@@ -218,7 +218,7 @@ def tile_rgchromahistblock_kernel(tc, x, out):
                 bank = ring.tile([P, 512], F32)
                 banks[u, q, k] = bank
                 n = 4 * (q % 2) + k
-                transposes(u, bank, [sq[u, q // 2]] + [n16[u]] * (n // 2) + [n8[u]] * (n % 2))
+                transposes(u, bank, [sq[u, q // 2]] + [n24[u]] * (n // 3) + [n8[u]] * (n % 3))
 
         def products(u, q):
             nb = nrows(u)
@@ -394,13 +394,13 @@ def tile_rgchromahistblock_kernel(tc, x, out):
         u, q = prior
         for job in jobs:
             done = done + multiply(job)
-        from_products(u, q, 0, nrows(u))
-        nb = nrows(u)
-        for e2 in range(2):
-            src = rr[u, q][e2][:, 0:nb]
-            nc.vector.tensor_tensor(out=kview(u, 0, nb, q)[:, :, 2 * e2], in0=src, in1=src, op=ALU.mult)
-        calls = calls + [(u, first) for first in range(0, PASSES_TILE * len(units[u]), QP)]
         for call in calls:
             done = done + multiply(quantise(call[0], call[1]))
+        for first in range(0, PASSES_TILE * len(units[u]), QP):
+            r0, r1 = 2 * first, 2 * (first + QP)
+            from_products(u, q, r0, r1)
+            for e2 in range(2):
+                nc.scalar.activation(out=kview(u, r0, r1, q)[:, :, 2 * e2], in_=rr[u, q][e2][:, r0:r1], func=ACTF.Square)
+            done = done + multiply(quantise(u, first))
         for kb in done:
             finish(kb)

@@ -30,7 +30,7 @@ CHUNKS = 4
 QP = 8
 SEEDS = (-4, 28)
 GA = 56
-SA = 106
+SA = 104
 
 FLOPS = 2 * IMAGES * PIXELS * BINS * BINS
 
@@ -224,8 +224,6 @@ def tile_rgchromahistblock_kernel(tc, x, out):
             nb = nrows(u)
             xq = xpool.tile([P, 2 * BT, 2, 16], F32)
             xx[u, q] = xq
-            if q == 0:
-                derive(u, 0)
             for k in range(4):
                 derive(u, 4 * q + k + 1)
                 for side in range(2):
@@ -261,15 +259,16 @@ def tile_rgchromahistblock_kernel(tc, x, out):
         def square_roots(u, q, part):
             c = cuts(u)
             nb = nrows(u)
+            src = rr[u, q][1][:, c[part]:c[part + 1]]
+            dst = kview(u, c[part], c[part + 1], q)[:, :, 2]
             if part == 0:
-                src = rr[u, q][1][:, 0:nb]
-                nc.gpsimd.tensor_tensor(out=kview(u, 0, nb, q)[:, :, 2], in0=src, in1=src, op=ALU.mult)
-            src = rr[u, q][0][:, c[part]:c[part + 1]]
-            dst = kview(u, c[part], c[part + 1], q)[:, :, 0]
-            if part == 1:
+                nc.gpsimd.tensor_tensor(out=dst, in0=src, in1=src, op=ALU.mult)
+                src = rr[u, q][0][:, 0:nb]
+                nc.gpsimd.tensor_tensor(out=kview(u, 0, nb, q)[:, :, 0], in0=src, in1=src, op=ALU.mult)
+            elif part == 1:
                 nc.scalar.activation(out=dst, in_=src, func=ACTF.Square)
             else:
-                (nc.vector if part == 2 else nc.gpsimd).tensor_tensor(out=dst, in0=src, in1=src, op=ALU.mult)
+                nc.vector.tensor_tensor(out=dst, in0=src, in1=src, op=ALU.mult)
 
         def finish(kb):
             hist = acc[kb][:].rearrange("p (i c) -> p i c", c=P)[:, :, BINS:P]
@@ -325,6 +324,7 @@ def tile_rgchromahistblock_kernel(tc, x, out):
         square(0, 0)
         chroma_bank(0)
         make_seeds(0)
+        derive(0, 0)
 
         calls = []
         jobs = []
@@ -369,24 +369,28 @@ def tile_rgchromahistblock_kernel(tc, x, out):
             if q == 1 and u >= 1:
                 calls = calls + [(u - 1, first) for first in range(0, PASSES_TILE * len(units[u - 1]), QP)]
             share = min(len(calls), 2)
-            for n in range(max(share, len(little))):
-                if n < len(little):
-                    little[n]()
-                if n < share:
-                    jobs.append(quantise(calls[n][0], calls[n][1]))
-                if n == 0 and prior is not None:
-                    square_roots(prior[0], prior[1], 2)
-            if max(share, len(little)) == 0 and prior is not None:
-                square_roots(prior[0], prior[1], 2)
+            quantisers = [lambda call=call: jobs.append(quantise(call[0], call[1])) for call in calls[0:share]]
             calls = calls[share:]
-            chain_roots(u, q)
-            for kb in finished:
-                finish(kb)
+            squares = [] if prior is None else [lambda: square_roots(prior[0], prior[1], 2)]
+            if q == 0:
+                work = little[0:1] + quantisers[0:1] + little[1:2] + quantisers[1:] + squares
+                behind = little[2:]
+            else:
+                work = little[0:1] + squares + little[1:2] + quantisers[:-1] + little[2:]
+                behind = quantisers[-1:]
+            for f in work:
+                f()
             if q == 0:
                 kh = kpool.tile([P, 2 * BT, 4 * BINS], BF16, align_bytes=64)
                 kt[u] = kh
-            if (u, q) != steps[-1]:
-                hold(u, q)
+            hold(u, q)
+            for f in behind:
+                f()
+            if q == 3 and not last:
+                derive(u + 1, 0)
+            chain_roots(u, q)
+            for kb in finished:
+                finish(kb)
             if q == 1 and u + 2 < len(units):
                 load(u + 2)
             prior = (u, q)

@@ -28,9 +28,10 @@ TSQ = S2 + 1.0
 KAPPA = 4.0 * S2 + 4.0
 CHUNKS = 4
 QP = 8
-SEEDS = (-4, 28)
+ORDER = (1, 0, 2, 3)
+MIDDLE = 32
 GA = 56
-SA = 104
+SA = 108
 
 FLOPS = 2 * IMAGES * PIXELS * BINS * BINS
 
@@ -56,6 +57,8 @@ def tile_rgchromahistblock_kernel(tc, x, out):
         ring = ctx.enter_context(tc.psum_pool(name="ring", bufs=4))
         ctx.enter_context(tc.manual_schedule())
 
+        identb = const.tile([P, P], BF16)
+        make_identity(nc, identb[:])
         ident = const.tile([P, P], F32)
         make_identity(nc, ident[:])
         identv = ident[:].rearrange("p (s t) -> p s t", t=4)
@@ -80,12 +83,12 @@ def tile_rgchromahistblock_kernel(tc, x, out):
             n = columns[value]
             return cbias[:, n:n + 1]
 
-        for value in ([-2.0, 4.0, -28.0, -34.0, -KAPPA / (S2 * S2), -1.0 / S2]
+        for value in ([EPS, -2.0, -float(MIDDLE), -34.0, -KAPPA / (S2 * S2), -1.0 / S2]
                       + [1.0 + bank_constant(k, q) / S2 for q in range(CHUNKS) for k in range(4)]):
             bias(value)
 
         units = [[2 * u + v for v in range(2) if 2 * u + v < TILES] for u in range((TILES + 1) // 2)]
-        steps = [(u, q) for u in range(len(units)) for q in range(CHUNKS)]
+        steps = [(u, q) for u in range(len(units)) for q in ORDER]
 
         xt = {}
         n8 = {}
@@ -117,8 +120,7 @@ def tile_rgchromahistblock_kernel(tc, x, out):
         def prepare(u):
             nt = len(units[u])
             cl = prep.tile([P, 2, 3, P], BF16)
-            s1 = prep.tile([P, 2, P], F32)
-            s2 = prep.tile([P, 2, P], F32)
+            e = prep.tile([P, 2, P], F32)
             m = prep.tile([P, 2, P], F32)
             y0 = prep.tile([P, 2, P], F32)
             t8 = lpool.tile([P, 2, 2, P], F32)
@@ -126,6 +128,13 @@ def tile_rgchromahistblock_kernel(tc, x, out):
             n8[u] = t8
             n24[u] = t24
             xs = xt[u]
+            bank = xps.tile([P, 512], F32)
+            xb[u] = bank
+            total = bank[:, 0:2 * P].rearrange("p (v n) -> p v n", v=2)[:, 0:nt]
+
+            def channel_sum():
+                for ch in range(3):
+                    nc.tensor.matmul(out=total, lhsT=identb[:], rhs=cl[:, 0:nt, ch, :], start=ch == 0, stop=ch == 2)
 
             def chroma(ch):
                 nc.vector.scalar_tensor_tensor(out=t8[:, 0:nt, ch, :], in0=cl[:, 0:nt, ch, :], scalar=504.0, in1=m[:, 0:nt],
@@ -135,14 +144,12 @@ def tile_rgchromahistblock_kernel(tc, x, out):
                 [
                     lambda: nc.vector.tensor_scalar(out=cl[:, 0:nt], in0=xs[:, 0:nt], scalar1=0.0, scalar2=1.0,
                                                     op0=ALU.max, op1=ALU.min),
-                    lambda: nc.vector.scalar_tensor_tensor(out=s1[:, 0:nt], in0=cl[:, 0:nt, 0, :], scalar=EPS,
-                                                           in1=cl[:, 0:nt, 1, :], op0=ALU.add, op1=ALU.add),
-                    lambda: nc.vector.tensor_tensor(out=s2[:, 0:nt], in0=s1[:, 0:nt], in1=cl[:, 0:nt, 2, :], op=ALU.add),
                 ],
                 [
                     lambda: nc.vector.tensor_tensor(out=y0[:, 0:nt], in0=m[:, 0:nt], in1=m[:, 0:nt], op=ALU.mult),
-                    lambda: nc.vector.tensor_tensor(out=s1[:, 0:nt], in0=s2[:, 0:nt], in1=y0[:, 0:nt], op=ALU.mult),
-                    lambda: nc.vector.scalar_tensor_tensor(out=m[:, 0:nt], in0=s1[:, 0:nt], scalar=2.0, in1=y0[:, 0:nt],
+                    lambda: nc.vector.scalar_tensor_tensor(out=e[:, 0:nt], in0=total, scalar=EPS, in1=y0[:, 0:nt],
+                                                           op0=ALU.add, op1=ALU.mult),
+                    lambda: nc.vector.scalar_tensor_tensor(out=m[:, 0:nt], in0=e[:, 0:nt], scalar=2.0, in1=y0[:, 0:nt],
                                                            op0=ALU.subtract, op1=ALU.mult),
                 ],
                 [
@@ -152,7 +159,8 @@ def tile_rgchromahistblock_kernel(tc, x, out):
                 ],
                 [],
             ]
-            return lambda: nc.scalar.activation(out=m[:, 0:nt], in_=s2[:, 0:nt], func=ACTF.Abs_reciprocal_sqrt, scale=1.0)
+            return channel_sum, lambda: nc.scalar.activation(out=m[:, 0:nt], in_=total, func=ACTF.Abs_reciprocal_sqrt,
+                                                             bias=bias(EPS), scale=1.0)
 
         def square(u, h):
             nt = len(units[u])
@@ -169,25 +177,37 @@ def tile_rgchromahistblock_kernel(tc, x, out):
                                          stop=n == len(sources) - 1, is_transpose=True)
 
         def chroma_bank(u):
-            bank = xps.tile([P, 512], F32)
-            xb[u] = bank
-            transposes(u, bank, [n8[u]])
+            transposes(u, xb[u], [n8[u]])
 
         def block(bank, nb):
             return bank[:, 0:4 * nb].rearrange("p (b t) -> p b t", t=4)
 
         def make_seeds(u):
             nb = nrows(u)
-            for i in SEEDS:
-                sd = small.tile([P, 512], F32, tag="seed%d" % (i + 4), name="seed")
-                seeds[u, i] = sd
-                nc.scalar.activation(out=sd[:, 0:4 * nb], in_=xb[u][:, 0:4 * nb], func=ACTF.Square, bias=bias(-float(i)), scale=-0.125)
+            sd = small.tile([P, 512], F32, tag="seed", name="seed")
+            seeds[u] = sd
+            nc.scalar.activation(out=sd[:, 0:4 * nb], in_=xb[u][:, 0:4 * nb], func=ACTF.Square, bias=bias(-float(MIDDLE)),
+                                 scale=-0.125)
+
+        def sign(q):
+            return -1.0 if q < 2 else 1.0
+
+        def start_down(u):
+            nb = nrows(u)
+            w = wpool.tile([P, 512], F32, tag="wend", bufs=1, name="wend")
+            ws[u, 5] = w
+            nc.vector.tensor_scalar(out=w[:, 0:4 * nb], in0=seeds[u][:, 0:4 * nb], scalar1=-1.0, scalar2=TSQ,
+                                    op0=ALU.mult, op1=ALU.subtract)
+
+        def start_up(u):
+            nb = nrows(u)
+            nc.vector.tensor_scalar(out=wslot(u, 8), in0=block(seeds[u], nb), scalar1=TSQ, scalar2=None, op0=ALU.add)
 
         def wslot(u, x4):
             nb = nrows(u)
             if x4 == 16:
                 if (u, 4) not in ws:
-                    w = wpool.tile([P, 512], F32, tag="wlast", bufs=1, name="wlast")
+                    w = wpool.tile([P, 512], F32, tag="wend", bufs=1, name="wend")
                     ws[u, 4] = w
                 return block(ws[u, 4], nb)
             q, k = divmod(x4, 4)
@@ -199,12 +219,8 @@ def tile_rgchromahistblock_kernel(tc, x, out):
         def derive(u, x4):
             nb = nrows(u)
             i = 4 * x4
-            add = float(8 * i - 16)
-            if i - 4 in SEEDS:
-                before = block(seeds[u, i - 4], nb)
-                add = add + TSQ
-            else:
-                before = wslot(u, x4 - 1)
+            add = float(8 * i + 16 if x4 < 8 else 8 * i - 16)
+            before = block(ws[u, 5], nb) if x4 == 7 else wslot(u, x4 + 1 if x4 < 8 else x4 - 1)
             nc.vector.scalar_tensor_tensor(out=wslot(u, x4), in0=block(xb[u], nb), scalar=add, in1=before,
                                            op0=ALU.add, op1=ALU.add)
 
@@ -213,8 +229,11 @@ def tile_rgchromahistblock_kernel(tc, x, out):
 
         banks = {}
 
+        def order(q):
+            return (0, 1, 2, 3) if q >= 2 else (3, 2, 1, 0)
+
         def fill(u, q):
-            for k in range(4):
+            for k in order(q):
                 bank = ring.tile([P, 512], F32)
                 banks[u, q, k] = bank
                 n = 4 * (q % 2) + k
@@ -224,16 +243,19 @@ def tile_rgchromahistblock_kernel(tc, x, out):
             nb = nrows(u)
             xq = xpool.tile([P, 2 * BT, 2, 16], F32)
             xx[u, q] = xq
-            for k in range(4):
-                derive(u, 4 * q + k + 1)
+            for k in order(q):
+                x4 = 4 * q + k + (1 if q >= 2 else -1)
+                if x4 >= 0:
+                    derive(u, x4)
                 for side in range(2):
                     nc.vector.scalar_tensor_tensor(
                         out=xq[:, 0:nb, side, 4 * k:4 * k + 4], in0=block(banks[u, q, k], nb), scalar=TSQ + bank_constant(k, q),
-                        in1=wslot(u, 4 * q + k + side), op0=ALU.add, op1=ALU.mult)
+                        in1=block(ws[u, 5], nb) if 4 * q + k + side == 8 and q < 2 else wslot(u, 4 * q + k + side),
+                        op0=ALU.add, op1=ALU.mult)
 
         def bank_root(u, q, k):
             nb = nrows(u)
-            if k == 0:
+            if k == order(q)[0]:
                 r2 = rpool.tile([P, 2 * BT, 16], F32, tag="r2", name="r2")
                 rr[u, q] = [None, r2]
             nc.scalar.activation(out=rr[u, q][1][:, 0:nb, 4 * k:4 * k + 4], in_=block(banks[u, q, k], nb),
@@ -244,11 +266,11 @@ def tile_rgchromahistblock_kernel(tc, x, out):
             r0 = rpool.tile([P, 2 * BT, 16], F32, tag="r0", bufs=1, name="r0")
             rr[u, q][0] = r0
             nc.scalar.activation(out=r0[:, 0:nb], in_=ws[u, q][:, 0:nb, :], func=ACTF.Abs_reciprocal_sqrt,
-                                 bias=bias(-1.0 / S2), scale=1.0 / S2)
+                                 bias=bias(-1.0 / S2), scale=sign(q) / S2)
 
         def from_products(u, q, r0, r1):
             nc.scalar.activation(out=kview(u, r0, r1, q)[:, :, 1::2], in_=xx[u, q][:, r0:r1], func=ACTF.Abs_reciprocal_sqrt,
-                                 bias=bias(-KAPPA / (S2 * S2)), scale=1.0 / (S2 * S2))
+                                 bias=bias(-KAPPA / (S2 * S2)), scale=sign(q) / (S2 * S2))
 
         def cuts(u):
             return [c * len(units[u]) // 2 for c in (0, GA, SA, 2 * BT)]
@@ -315,16 +337,18 @@ def tile_rgchromahistblock_kernel(tc, x, out):
 
         load(0)
         load(1)
-        root = prepare(0)
+        channel_sum, root = prepare(0)
         for f in stages[0][0]:
             f()
+        channel_sum()
         root()
         for f in stages[0][1] + stages[0][2]:
             f()
         square(0, 0)
         chroma_bank(0)
         make_seeds(0)
-        derive(0, 0)
+        start_down(0)
+        derive(0, 7)
 
         calls = []
         jobs = []
@@ -333,13 +357,17 @@ def tile_rgchromahistblock_kernel(tc, x, out):
         prior = None
         for u, q in steps:
             last = u == len(units) - 1
-            if q == 0 and not last:
-                root = prepare(u + 1)
+            place = ORDER.index(q)
+            ks = order(q)
+            if place == 0 and not last:
+                channel_sum, root = prepare(u + 1)
             fill(u, q)
             for job in jobs:
                 done = done + multiply(job)
             jobs = []
-            if q == 3 and not last:
+            if place == 1 and not last:
+                channel_sum()
+            if place == 3 and not last:
                 chroma_bank(u + 1)
             if prior is not None:
                 square_roots(prior[0], prior[1], 0)
@@ -348,50 +376,52 @@ def tile_rgchromahistblock_kernel(tc, x, out):
             if prior is not None:
                 half = nrows(prior[0]) // 2
                 from_products(prior[0], prior[1], 0, half)
-            bank_root(u, q, 0)
+            bank_root(u, q, ks[0])
             if prior is not None:
                 square_roots(prior[0], prior[1], 1)
-            if q == 1 and not last:
+            if place == 1 and not last:
                 root()
-            bank_root(u, q, 1)
-            if q == 1:
+            bank_root(u, q, ks[1])
+            if place == 1:
                 square(u, 1)
-            elif q == 3 and not last:
+            elif place == 3 and not last:
                 square(u + 1, 0)
                 make_seeds(u + 1)
             if prior is not None:
                 from_products(prior[0], prior[1], half, 2 * half)
-            bank_root(u, q, 2)
-            bank_root(u, q, 3)
+            bank_root(u, q, ks[2])
+            bank_root(u, q, ks[3])
             finished = done
             done = []
-            little = [] if last else stages[u + 1][q]
-            if q == 1 and u >= 1:
+            little = [] if last else list(stages[u + 1][place])
+            if place == 1:
+                little.append(lambda: start_up(u))
+            if place == 3 and not last:
+                little = [lambda: start_down(u + 1), lambda: derive(u + 1, 7)]
+            if place == 1 and u >= 1:
                 calls = calls + [(u - 1, first) for first in range(0, PASSES_TILE * len(units[u - 1]), QP)]
             share = min(len(calls), 2)
             quantisers = [lambda call=call: jobs.append(quantise(call[0], call[1])) for call in calls[0:share]]
             calls = calls[share:]
             squares = [] if prior is None else [lambda: square_roots(prior[0], prior[1], 2)]
-            if q == 0:
-                work = little[0:1] + quantisers[0:1] + little[1:2] + quantisers[1:] + squares
-                behind = little[2:]
+            if place == 0:
+                work = little[0:1] + quantisers[0:1] + little[1:2] + quantisers[1:]
+                behind = squares + little[2:]
             else:
                 work = little[0:1] + squares + little[1:2] + quantisers[:-1] + little[2:]
                 behind = quantisers[-1:]
             for f in work:
                 f()
-            if q == 0:
+            if place == 0:
                 kh = kpool.tile([P, 2 * BT, 4 * BINS], BF16, align_bytes=64)
                 kt[u] = kh
             hold(u, q)
             for f in behind:
                 f()
-            if q == 3 and not last:
-                derive(u + 1, 0)
             chain_roots(u, q)
             for kb in finished:
                 finish(kb)
-            if q == 1 and u + 2 < len(units):
+            if place == 1 and u + 2 < len(units):
                 load(u + 2)
             prior = (u, q)
 

@@ -362,13 +362,13 @@ def tile_rgchromahistblock_kernel(tc, x, out):
             if place == 0 and not last:
                 channel_sum, root = prepare(u + 1)
             fill(u, q)
-            for job in jobs:
-                done = done + multiply(job)
-            jobs = []
             if place == 1 and not last:
                 channel_sum()
             if place == 3 and not last:
                 chroma_bank(u + 1)
+            for job in jobs:
+                done = done + multiply(job)
+            jobs = []
             if prior is not None:
                 square_roots(prior[0], prior[1], 0)
             products(u, q)

from contextlib import ExitStack

import concourse.mybir as mybir
from concourse.masks import make_identity

F32 = mybir.dt.float32
BF16 = mybir.dt.bfloat16
U32 = mybir.dt.uint32
U8 = mybir.dt.uint8
FP8X4 = mybir.dt.float8_e4m3fn_x4
ALU = mybir.AluOpType
ACTF = mybir.ActivationFunctionType
AX = mybir.AxisListType

P = 128
IMAGES = 16
PIXELS = 224 * 224
BINS = 64
EPS = 1e-6
SIGMA = 0.02
ROWS = PIXELS // P
TILES = IMAGES * ROWS // P
PASSES_TILE = P // 4
PASSES_IMAGE = ROWS // 4
BT = 2 * PASSES_TILE
S2 = (63.0 * SIGMA) ** 2
TSQ = S2 + 1.0
KAPPA = 4.0 * S2 + 4.0
CHUNKS = 4
QP = 8
ORDER = (1, 0, 2, 3)
MIDDLE = 32
GA = 56
SA = 108

FLOPS = 2 * IMAGES * PIXELS * BINS * BINS


def tile_rgchromahistblock_kernel(tc, x, out):
    nc = tc.nc
    xv = x.rearrange("b c h w -> b c (h w)").rearrange("b c (r w) -> b r c w", w=P)
    outv = out.rearrange("b o (y g) j -> g y (b o) j", g=4)
    with ExitStack() as ctx:
        const = ctx.enter_context(tc.tile_pool(name="const", bufs=1))
        xin = ctx.enter_context(tc.tile_pool(name="xin", bufs=2))
        prep = ctx.enter_context(tc.tile_pool(name="prep", bufs=1))
        lpool = ctx.enter_context(tc.tile_pool(name="lpool", bufs=2))
        sqpool = ctx.enter_context(tc.tile_pool(name="sqpool", bufs=2))
        wpool = ctx.enter_context(tc.tile_pool(name="wpool", bufs=2))
        xpool = ctx.enter_context(tc.tile_pool(name="xpool", bufs=2))
        rpool = ctx.enter_context(tc.tile_pool(name="rpool", bufs=2))
        kpool = ctx.enter_context(tc.tile_pool(name="kpool", bufs=2))
        cpool = ctx.enter_context(tc.tile_pool(name="cpool", bufs=2))
        small = ctx.enter_context(tc.tile_pool(name="small", bufs=1))
        accp = ctx.enter_context(tc.psum_pool(name="accp", bufs=2))
        xps = ctx.enter_context(tc.psum_pool(name="xps", bufs=2))
        ring = ctx.enter_context(tc.psum_pool(name="ring", bufs=4))
        ctx.enter_context(tc.manual_schedule())

        identb = const.tile([P, P], BF16)
        make_identity(nc, identb[:])
        ident = const.tile([P, P], F32)
        make_identity(nc, ident[:])
        identv = ident[:].rearrange("p (s t) -> p s t", t=4)
        sel = const.tile([P, P], F32)
        nc.vector.memset(sel[0:64, :], 1.0)
        nc.vector.memset(sel[64:128, :], 0.0)
        zero = const.tile([P, 1], F32)
        nc.vector.memset(zero[:], 0.0)
        cbias = const.tile([P, 32], F32)
        columns = {}

        def bank_constant(k, q):
            h, odd = divmod(q, 2)
            m = 16 * odd + 4 * k
            return float(2 * m * (32 * h + 2) + m * m)

        def bias(value):
            if value not in columns:
                n = len(columns)
                nc.vector.tensor_scalar(out=cbias[:, n:n + 1], in0=zero[:], scalar1=value, scalar2=None, op0=ALU.add)
                columns[value] = n
            n = columns[value]
            return cbias[:, n:n + 1]

        for value in ([EPS, -2.0, -float(MIDDLE), -34.0, -KAPPA / (S2 * S2), -1.0 / S2]
                      + [1.0 + bank_constant(k, q) / S2 for q in range(CHUNKS) for k in range(4)]):
            bias(value)

        units = [[2 * u + v for v in range(2) if 2 * u + v < TILES] for u in range((TILES + 1) // 2)]
        steps = [(u, q) for u in range(len(units)) for q in ORDER]

        xt = {}
        n8 = {}
        n24 = {}
        sq = {}
        xb = {}
        seeds = {}
        ws = {}
        xx = {}
        rr = {}
        kt = {}
        acc = {}
        stages = {}

        def nrows(u):
            return BT * len(units[u])

        def load(u):
            xu = xin.tile([P, 2, 3, P], BF16)
            xt[u] = xu
            for v, tile in enumerate(units[u]):
                done = 0
                while done < P:
                    b, r = divmod(tile * P + done, ROWS)
                    n = min(P - done, ROWS - r)
                    nc.sync.dma_start(out=xu[done:done + n, v], in_=xv[b, r:r + n])
                    done += n

        def prepare(u):
            nt = len(units[u])
            cl = prep.tile([P, 2, 3, P], BF16)
            e = prep.tile([P, 2, P], F32)
            m = prep.tile([P, 2, P], F32)
            y0 = prep.tile([P, 2, P], F32)
            t8 = lpool.tile([P, 2, 2, P], F32)
            t24 = lpool.tile([P, 2, 2, P], F32)
            n8[u] = t8
            n24[u] = t24
            xs = xt[u]
            bank = xps.tile([P, 512], F32)
            xb[u] = bank
            total = bank[:, 0:2 * P].rearrange("p (v n) -> p v n", v=2)[:, 0:nt]

            def channel_sum():
                for ch in range(3):
                    nc.tensor.matmul(out=total, lhsT=identb[:], rhs=cl[:, 0:nt, ch, :], start=ch == 0, stop=ch == 2)

            def chroma(ch):
                nc.vector.scalar_tensor_tensor(out=t8[:, 0:nt, ch, :], in0=cl[:, 0:nt, ch, :], scalar=504.0, in1=m[:, 0:nt],
                                               op0=ALU.mult, op1=ALU.mult)

            stages[u] = [
                [
                    lambda: nc.vector.tensor_scalar(out=cl[:, 0:nt], in0=xs[:, 0:nt], scalar1=0.0, scalar2=1.0,
                                                    op0=ALU.max, op1=ALU.min),
                ],
                [
                    lambda: nc.vector.tensor_tensor(out=y0[:, 0:nt], in0=m[:, 0:nt], in1=m[:, 0:nt], op=ALU.mult),
                    lambda: nc.vector.scalar_tensor_tensor(out=e[:, 0:nt], in0=total, scalar=EPS, in1=y0[:, 0:nt],
                                                           op0=ALU.add, op1=ALU.mult),
                    lambda: nc.vector.scalar_tensor_tensor(out=m[:, 0:nt], in0=e[:, 0:nt], scalar=2.0, in1=y0[:, 0:nt],
                                                           op0=ALU.subtract, op1=ALU.mult),
                ],
                [
                    lambda: chroma(0),
                    lambda: chroma(1),
                    lambda: nc.vector.tensor_scalar(out=t24[:, 0:nt], in0=t8[:, 0:nt], scalar1=3.0, scalar2=None, op0=ALU.mult),
                ],
                [],
            ]
            return channel_sum, lambda: nc.scalar.activation(out=m[:, 0:nt], in_=total, func=ACTF.Abs_reciprocal_sqrt,
                                                             bias=bias(EPS), scale=1.0)

        def square(u, h):
            nt = len(units[u])
            t = sqpool.tile([P, 2, 2, P], F32)
            sq[u, h] = t
            nc.scalar.activation(out=t[:, 0:nt], in_=n8[u][:, 0:nt], func=ACTF.Square, bias=bias(-float(32 * h + 2)), scale=-0.125)

        def transposes(u, bank, sources):
            view = bank[:].rearrange("p (v s c t) -> p v c s t", v=2, c=2, t=4)
            for v in range(len(units[u])):
                for ch in range(2):
                    for n, src in enumerate(sources):
                        nc.tensor.matmul(out=view[:, v, ch], lhsT=src[:, v, ch, :], rhs=identv, start=n == 0,
                                         stop=n == len(sources) - 1, is_transpose=True)

        def chroma_bank(u):
            transposes(u, xb[u], [n8[u]])

        def block(bank, nb):
            return bank[:, 0:4 * nb].rearrange("p (b t) -> p b t", t=4)

        def make_seeds(u):
            nb = nrows(u)
            sd = small.tile([P, 512], F32, tag="seed", name="seed")
            seeds[u] = sd
            nc.scalar.activation(out=sd[:, 0:4 * nb], in_=xb[u][:, 0:4 * nb], func=ACTF.Square, bias=bias(-float(MIDDLE)),
                                 scale=-0.125)

        def sign(q):
            return -1.0 if q < 2 else 1.0

        def start_down(u):
            nb = nrows(u)
            w = wpool.tile([P, 512], F32, tag="wend", bufs=1, name="wend")
            ws[u, 5] = w
            nc.vector.tensor_scalar(out=w[:, 0:4 * nb], in0=seeds[u][:, 0:4 * nb], scalar1=-1.0, scalar2=TSQ,
                                    op0=ALU.mult, op1=ALU.subtract)

        def start_up(u):
            nb = nrows(u)
            nc.vector.tensor_scalar(out=wslot(u, 8), in0=block(seeds[u], nb), scalar1=TSQ, scalar2=None, op0=ALU.add)

        def wslot(u, x4):
            nb = nrows(u)
            if x4 == 16:
                if (u, 4) not in ws:
                    w = wpool.tile([P, 512], F32, tag="wend", bufs=1, name="wend")
                    ws[u, 4] = w
                return block(ws[u, 4], nb)
            q, k = divmod(x4, 4)
            if (u, q) not in ws:
                w = wpool.tile([P, 2 * BT, 16], F32, tag="ws", name="ws")
                ws[u, q] = w
            return ws[u, q][:, 0:nb, 4 * k:4 * k + 4]

        def derive(u, x4):
            nb = nrows(u)
            i = 4 * x4
            add = float(8 * i + 16 if x4 < 8 else 8 * i - 16)
            before = block(ws[u, 5], nb) if x4 == 7 else wslot(u, x4 + 1 if x4 < 8 else x4 - 1)
            nc.vector.scalar_tensor_tensor(out=wslot(u, x4), in0=block(xb[u], nb), scalar=add, in1=before,
                                           op0=ALU.add, op1=ALU.add)

        def kview(u, r0, r1, q):
            return kt[u][:].rearrange("p b (g q e) -> p b g q e", g=4, q=4)[:, r0:r1, :, q, :]

        banks = {}

        def order(q):
            return (0, 1, 2, 3) if q >= 2 else (3, 2, 1, 0)

        def fill(u, q):
            for k in order(q):
                bank = ring.tile([P, 512], F32)
                banks[u, q, k] = bank
                n = 4 * (q % 2) + k
                transposes(u, bank, [sq[u, q // 2]] + [n24[u]] * (n // 3) + [n8[u]] * (n % 3))

        def products(u, q):
            nb = nrows(u)
            xq = xpool.tile([P, 2 * BT, 2, 16], F32)
            xx[u, q] = xq
            for k in order(q):
                x4 = 4 * q + k + (1 if q >= 2 else -1)
                if x4 >= 0:
                    derive(u, x4)
                for side in range(2):
                    nc.vector.scalar_tensor_tensor(
                        out=xq[:, 0:nb, side, 4 * k:4 * k + 4], in0=block(banks[u, q, k], nb), scalar=TSQ + bank_constant(k, q),
                        in1=block(ws[u, 5], nb) if 4 * q + k + side == 8 and q < 2 else wslot(u, 4 * q + k + side),
                        op0=ALU.add, op1=ALU.mult)

        def bank_root(u, q, k):
            nb = nrows(u)
            if k == order(q)[0]:
                r2 = rpool.tile([P, 2 * BT, 16], F32, tag="r2", name="r2")
                rr[u, q] = [None, r2]
            nc.scalar.activation(out=rr[u, q][1][:, 0:nb, 4 * k:4 * k + 4], in_=block(banks[u, q, k], nb),
                                 func=ACTF.Abs_reciprocal_sqrt, bias=bias(1.0 + bank_constant(k, q) / S2), scale=1.0 / S2)

        def chain_roots(u, q):
            nb = nrows(u)
            r0 = rpool.tile([P, 2 * BT, 16], F32, tag="r0", bufs=1, name="r0")
            rr[u, q][0] = r0
            nc.scalar.activation(out=r0[:, 0:nb], in_=ws[u, q][:, 0:nb, :], func=ACTF.Abs_reciprocal_sqrt,
                                 bias=bias(-1.0 / S2), scale=sign(q) / S2)

        def from_products(u, q, r0, r1):
            nc.scalar.activation(out=kview(u, r0, r1, q)[:, :, 1::2], in_=xx[u, q][:, r0:r1], func=ACTF.Abs_reciprocal_sqrt,
                                 bias=bias(-KAPPA / (S2 * S2)), scale=sign(q) / (S2 * S2))

        def cuts(u):
            return [c * len(units[u]) // 2 for c in (0, GA, SA, 2 * BT)]

        def hold(u, q):
            nc.vector.memset(kview(u, 0, 1, q)[:, 0, 2, :], 0.0)

        def square_roots(u, q, part):
            c = cuts(u)
            nb = nrows(u)
            src = rr[u, q][1][:, c[part]:c[part + 1]]
            dst = kview(u, c[part], c[part + 1], q)[:, :, 2]
            if part == 0:
                nc.gpsimd.tensor_tensor(out=dst, in0=src, in1=src, op=ALU.mult)
                src = rr[u, q][0][:, 0:nb]
                nc.gpsimd.tensor_tensor(out=kview(u, 0, nb, q)[:, :, 0], in0=src, in1=src, op=ALU.mult)
            elif part == 1:
                nc.scalar.activation(out=dst, in_=src, func=ACTF.Square)
            else:
                nc.vector.tensor_tensor(out=dst, in0=src, in1=src, op=ALU.mult)

        def finish(kb):
            hist = acc[kb][:].rearrange("p (i c) -> p i c", c=P)[:, :, BINS:P]
            rsum = small.tile([P, 4], F32)
            nc.vector.tensor_reduce(out=rsum[:], in_=hist, axis=AX.X, op=ALU.add)
            tot = ring.tile([P, 512], F32, tag="bank", name="bank")
            nc.tensor.matmul(out=tot[:, 0:4], lhsT=sel[:], rhs=rsum[:], start=True, stop=True)
            te = small.tile([P, 4], F32)
            nc.vector.tensor_scalar(out=te[:], in0=tot[:, 0:4], scalar1=EPS, scalar2=None, op0=ALU.add)
            rt = small.tile([P, 4], F32)
            nc.vector.reciprocal(out=rt[:], in_=te[:])
            o = small.tile([BINS, 4, BINS], F32)
            for i in range(4):
                nc.vector.tensor_scalar(out=o[:, i, :].rearrange("p (y g) -> p g y", g=4),
                                        in0=hist[0:BINS, i, :].rearrange("p (g y) -> p g y", g=4),
                                        scalar1=rt[0:BINS, i:i + 1], scalar2=None, op0=ALU.mult)
            for g in range(4):
                nc.sync.dma_start(out=outv[g, :, 4 * kb:4 * kb + 4, :], in_=o[16 * g:16 * g + 16])

        def quantise(u, first):
            codes = cpool.tile([P, QP * P], U32, align_bytes=64)
            scales = cpool.tile([P, QP * P], U8, align_bytes=64)
            nc.vector.quantize_mx(out=codes[:].bitcast(FP8X4), scales=scales[:],
                                  in_=kt[u][:, 2 * first:2 * (first + QP), :].rearrange("p b e -> p (b e)"))
            return (u, first, codes, scales)

        def multiply(job):
            u, first, codes, scales = job
            complete = []
            for c in range(QP):
                b, n = divmod(units[u][0] * PASSES_TILE + first + c, PASSES_IMAGE)
                if b % 4 == 0 and n == 0:
                    a = accp.tile([P, 512], F32)
                    acc[b // 4] = a
                cols = slice(c * P, (c + 1) * P)
                nc.tensor.matmul_mx(
                    out=acc[b // 4][:, (b % 4) * P:(b % 4 + 1) * P],
                    lhsT=codes[:, cols].bitcast(FP8X4), lhsT_scale=scales[:, cols],
                    rhs=codes[:, cols].bitcast(FP8X4), rhs_scale=scales[:, cols],
                    start=n == 0, stop=n == PASSES_IMAGE - 1)
                if b % 4 == 3 and n == PASSES_IMAGE - 1:
                    complete.append(b // 4)
            return complete

        load(0)
        load(1)
        channel_sum, root = prepare(0)
        for f in stages[0][0]:
            f()
        channel_sum()
        root()
        for f in stages[0][1] + stages[0][2]:
            f()
        square(0, 0)
        chroma_bank(0)
        make_seeds(0)
        start_down(0)
        derive(0, 7)

        calls = []
        jobs = []
        done = []
        root = None
        prior = None
        for u, q in steps:
            last = u == len(units) - 1
            place = ORDER.index(q)
            ks = order(q)
            if place == 0 and not last:
                channel_sum, root = prepare(u + 1)
            fill(u, q)
            if place == 1 and not last:
                channel_sum()
            if place == 3 and not last:
                chroma_bank(u + 1)
            for job in jobs:
                done = done + multiply(job)
            jobs = []
            if prior is not None:
                square_roots(prior[0], prior[1], 0)
            products(u, q)
            half = 0
            if prior is not None:
                half = nrows(prior[0]) // 2
                from_products(prior[0], prior[1], 0, half)
            bank_root(u, q, ks[0])
            if prior is not None:
                square_roots(prior[0], prior[1], 1)
            if place == 1 and not last:
                root()
            bank_root(u, q, ks[1])
            if place == 1:
                square(u, 1)
            elif place == 3 and not last:
                square(u + 1, 0)
                make_seeds(u + 1)
            if prior is not None:
                from_products(prior[0], prior[1], half, 2 * half)
            bank_root(u, q, ks[2])
            bank_root(u, q, ks[3])
            finished = done
            done = []
            little = [] if last else list(stages[u + 1][place])
            if place == 1:
                little.append(lambda: start_up(u))
            if place == 3 and not last:
                little = [lambda: start_down(u + 1), lambda: derive(u + 1, 7)]
            if place == 1 and u >= 1:
                calls = calls + [(u - 1, first) for first in range(0, PASSES_TILE * len(units[u - 1]), QP)]
            share = min(len(calls), 2)
            quantisers = [lambda call=call: jobs.append(quantise(call[0], call[1])) for call in calls[0:share]]
            calls = calls[share:]
            squares = [] if prior is None else [lambda: square_roots(prior[0], prior[1], 2)]
            if place == 0:
                work = little[0:1] + quantisers[0:1] + little[1:2] + quantisers[1:]
                behind = squares + little[2:]
            else:
                work = little[0:1] + squares + little[1:2] + quantisers[:-1] + little[2:]
                behind = quantisers[-1:]
            for f in work:
                f()
            if place == 0:
                kh = kpool.tile([P, 2 * BT, 4 * BINS], BF16, align_bytes=64)
                kt[u] = kh
            hold(u, q)
            for f in behind:
                f()
            chain_roots(u, q)
            for kb in finished:
                finish(kb)
            if place == 1 and u + 2 < len(units):
                load(u + 2)
            prior = (u, q)

        u, q = prior
        for job in jobs:
            done = done + multiply(job)
        for call in calls:
            done = done + multiply(quantise(call[0], call[1]))
        for first in range(0, PASSES_TILE * len(units[u]), QP):
            r0, r1 = 2 * first, 2 * (first + QP)
            from_products(u, q, r0, r1)
            for e2 in range(2):
                nc.scalar.activation(out=kview(u, r0, r1, q)[:, :, 2 * e2], in_=rr[u, q][e2][:, r0:r1], func=ACTF.Square)
            done = done + multiply(quantise(u, first))
        for kb in done:
            finish(kb)
